import numpy as np
import ml_dtypes


def mxq(x, axis, fmt="e4m3"):
    dtype, down = {"e4m3": (ml_dtypes.float8_e4m3fn, 7), "e5m2": (ml_dtypes.float8_e5m2, 14)}[fmt]
    v = np.moveaxis(np.asarray(x, np.float32).astype(ml_dtypes.bfloat16).astype(np.float64), axis, -1)
    blocks = v.reshape(v.shape[:-1] + (-1, 32))
    amax = np.abs(blocks).max(-1, keepdims=True)
    byte = np.maximum(np.where(amax > 0, np.frexp(amax)[1] - 1 + 127, 0) - down, 1)
    scale = np.exp2(byte - 127.0)
    codes = (blocks / scale).astype(np.float32).astype(dtype).astype(np.float64)
    return np.moveaxis((codes * scale).reshape(v.shape), -1, axis)


WIDE = False


def mx_kscale(k):
    if not WIDE:
        return np.ones(k)
    levels = np.array([10, -10, 5, -5, 0])
    a = np.random.permutation(np.resize(levels, k // 512 * 4)).reshape(k // 512, 4)
    idx = np.arange(k)
    return np.exp2(a[idx // 512, idx % 128 // 32])


BF16 = ml_dtypes.bfloat16


def bf(x):
    return np.asarray(x, np.float32).astype(BF16)


def f64(x):
    return np.asarray(x).astype(np.float64)


B, Lt, La, Dt, Da, H = 2, 512, 512, 1024, 1024, 1024
F = Dt + Da


def setup_inputs():
    u = mx_kscale(F)
    return {
        "scores": bf(np.random.standard_normal((B, Lt, La)) * 3.0),
        "auxiliary": bf(np.random.standard_normal((B, La, Da)) * u[Dt:]),
        "target": bf(np.random.standard_normal((B, Lt, Dt)) * u[:Dt]),
        "Wf": bf(np.random.standard_normal((F, Dt)) / np.sqrt(F) / u[:, None]),
        "b_f": bf(np.random.standard_normal(Dt) * 0.1),
    }


def reference(scores, auxiliary, target, Wf, b_f):
    sc = f64(scores)
    e = np.exp(sc - sc.max(-1, keepdims=True))
    attn = e / e.sum(-1, keepdims=True)
    weighted_aux = mxq(attn, 2, "e4m3") @ mxq(f64(auxiliary), 1, "e4m3")
    x = np.concatenate([f64(target), weighted_aux], axis=-1)
    y = np.tanh((mxq(x, 2, "e4m3") @ mxq(f64(Wf), 0, "e4m3")) + f64(b_f))
    return y.transpose(0, 2, 1)

@@ -1,0 +1,225 @@
+from contextlib import ExitStack
+
+import concourse.mybir as mybir
+from concourse.masks import make_identity
+
+BF16 = mybir.dt.bfloat16
+F32 = mybir.dt.float32
+U32 = mybir.dt.uint32
+U8 = mybir.dt.uint8
+FP8X4 = mybir.dt.float8_e4m3fn_x4
+ACT = mybir.ActivationFunctionType
+ALU = mybir.AluOpType
+AXIS = mybir.AxisListType
+
+P = 128
+PACK = 4
+K_PASS = P * PACK
+
+B = 2
+LT = 512
+LA = 512
+DT = 1024
+DA = 1024
+F = DT + DA
+T_TILES = LT // P
+N_TILES = DT // P
+G_ALL = F // K_PASS
+G_TGT = DT // K_PASS
+G_AUX = DA // K_PASS
+RUN = 4
+
+FLOPS = 2 * B * LT * LA * DA + 2 * B * LT * F * DT
+
+
+def tile_informationfusion_pb_kernel(tc, scores, auxiliary, target, Wf, b_f, out):
+    nc = tc.nc
+    with ExitStack() as ctx:
+        const = ctx.enter_context(tc.tile_pool(name="const", bufs=1))
+        raw = ctx.enter_context(tc.tile_pool(name="raw", bufs=1))
+        keep = ctx.enter_context(tc.tile_pool(name="keep", bufs=1))
+        soft = ctx.enter_context(tc.tile_pool(name="soft", bufs=4))
+        small_grp = ctx.enter_context(tc.tile_pool(name="small_grp", bufs=3))
+        grp = ctx.enter_context(tc.tile_pool(name="grp", bufs=3))
+        pooled_grp = ctx.enter_context(tc.tile_pool(name="pooled_grp", bufs=B * G_AUX))
+        result = ctx.enter_context(tc.tile_pool(name="result", bufs=4))
+        psum_tr = ctx.enter_context(tc.psum_pool(name="psum_tr", bufs=3))
+        psum_pool = ctx.enter_context(tc.psum_pool(name="psum_pool", bufs=2))
+        psum_acc = ctx.enter_context(tc.psum_pool(name="psum_acc", bufs=3))
+
+        ident_bf = const.tile([P, P], BF16)
+        make_identity(nc, ident_bf[:])
+        ident_f32 = const.tile([P, P], F32)
+        make_identity(nc, ident_f32[:])
+        bias_rows = const.tile([P, P], BF16)
+        nc.vector.memset(bias_rows[:], 0.0)
+
+        sc_raw = []
+        aux_raw = []
+        tgt_raw = []
+        for b in range(B):
+            sc_raw.append(raw.tile([P, T_TILES, LA], BF16, name="sc_raw%d" % b))
+            aux_raw.append(raw.tile([P, PACK, DA], BF16, name="aux_raw%d" % b))
+            tgt_raw.append(raw.tile([P, T_TILES * DT], BF16, name="tgt_raw%d" % b))
+        wf_raw = raw.tile([P, G_ALL, PACK, DT], BF16)
+
+        for b in range(B):
+            nc.sync.dma_start(out=sc_raw[b][:], in_=scores[b].rearrange("(tt p) a -> p tt a", p=P))
+            nc.sync.dma_start(out=aux_raw[b][:], in_=auxiliary[b].rearrange("(s p) d -> p s d", p=P))
+        nc.sync.dma_start(out=bias_rows[0:N_TILES, :], in_=b_f.rearrange("(i c) -> i c", c=P))
+        for b in range(B):
+            nc.sync.dma_start(
+                out=tgt_raw[b][:].rearrange("p (tt k) -> p tt k", k=DT),
+                in_=target[b].rearrange("(tt p) k -> p tt k", p=P),
+            )
+        for g in range(G_ALL):
+            rows = Wf[g * K_PASS : (g + 1) * K_PASS, :]
+            if g < G_TGT:
+                nc.sync.dma_start(
+                    out=wf_raw[:, g, :, :].rearrange("p (u e) n -> p u (e n)", e=2),
+                    in_=rows.rearrange("(u p e) n -> p u (e n)", p=P, e=2),
+                )
+            else:
+                nc.sync.dma_start(out=wf_raw[:, g, :, :], in_=rows.rearrange("(s p) n -> p s n", p=P))
+
+        at_codes, at_scales, aux_codes, aux_scales, x_codes, x_scales = [], [], [], [], [], []
+        for b in range(B):
+            at_codes.append(keep.tile([P, LT], U32, name="at_codes%d" % b, align_bytes=64))
+            at_scales.append(keep.tile([P, LT], U8, name="at_scales%d" % b, align_bytes=64))
+            aux_codes.append(keep.tile([P, DA], U32, name="aux_codes%d" % b, align_bytes=64))
+            aux_scales.append(keep.tile([P, DA], U8, name="aux_scales%d" % b, align_bytes=64))
+            x_codes.append(keep.tile([P, G_ALL, LT], U32, name="x_codes%d" % b, align_bytes=64))
+            x_scales.append(keep.tile([P, G_ALL, LT], U8, name="x_scales%d" % b, align_bytes=64))
+        wf_codes = keep.tile([P, N_TILES, G_ALL * P], U32, align_bytes=64)
+        wf_scales = keep.tile([P, N_TILES, G_ALL * P], U8, align_bytes=64)
+
+        neg_max = const.tile([P, B * T_TILES], F32)
+        row_sum = const.tile([P, B * T_TILES], F32)
+        inv_sum = const.tile([P, B * T_TILES], F32)
+
+        bias_ps = psum_tr.tile([P, P], BF16, tag="tr")
+        nc.tensor.transpose(bias_ps[:], bias_rows[:], ident_bf[:])
+        bias_col = const.tile([P, N_TILES], F32)
+        nc.vector.tensor_copy(out=bias_col[:], in_=bias_ps[:, 0:N_TILES])
+
+        def attention_tile(b, tt):
+            col = slice(b * T_TILES + tt, b * T_TILES + tt + 1)
+            t_cols = slice(tt * P, (tt + 1) * P)
+            rows = sc_raw[b][:, tt, :]
+            nc.vector.tensor_reduce(out=neg_max[:, col], in_=rows, axis=AXIS.X, op=ALU.max, negate=True)
+            e = soft.tile([P, LA], F32)
+            nc.scalar.activation(
+                out=e[:], in_=rows, func=ACT.Exp, bias=neg_max[:, col], scale=1.0, accum_out=row_sum[:, col]
+            )
+            nc.vector.reciprocal(out=inv_sum[:, col], in_=row_sum[:, col])
+            attn = soft.tile([P, LA], BF16)
+            nc.vector.tensor_scalar(out=attn[:], in0=e[:], scalar1=inv_sum[:, col], scalar2=None, op0=ALU.mult)
+            at_ps = psum_tr.tile([P, PACK, P], BF16, tag="tr")
+            for s in range(PACK):
+                nc.tensor.transpose(at_ps[:, s, :], attn[:, s * P : (s + 1) * P], ident_bf[:])
+            at_grp = small_grp.tile([P, P * PACK], BF16, align_bytes=64)
+            nc.scalar.copy(
+                out=at_grp[:].rearrange("p (t s) -> p t s", s=PACK), in_=at_ps[:].rearrange("p s t -> p t s")
+            )
+            nc.vector.quantize_mx(
+                out=at_codes[b][:, t_cols].bitcast(FP8X4), scales=at_scales[b][:, t_cols], in_=at_grp[:]
+            )
+
+        def quantise_auxiliary(b):
+            half = DA // 2
+            for h in range(2):
+                d_cols = slice(h * half, (h + 1) * half)
+                aux_grp = grp.tile([P, half * PACK], BF16, tag="grp", align_bytes=64)
+                nc.vector.tensor_copy(
+                    out=aux_grp[:].rearrange("p (c r s) -> p c s r", r=RUN, s=PACK),
+                    in_=aux_raw[b][:, :, d_cols].rearrange("p s (c r) -> p c s r", r=RUN),
+                )
+                nc.vector.quantize_mx(
+                    out=aux_codes[b][:, d_cols].bitcast(FP8X4), scales=aux_scales[b][:, d_cols], in_=aux_grp[:]
+                )
+
+        def pool_tile(b, tt, pooled):
+            t_cols = slice(tt * P, (tt + 1) * P)
+            for q in range(G_AUX):
+                wa_ps = psum_pool.tile([P, PACK, P], F32)
+                for s in range(PACK):
+                    d_cols = slice((q * PACK + s) * P, (q * PACK + s + 1) * P)
+                    nc.tensor.matmul_mx(
+                        out=wa_ps[:, s, :],
+                        lhsT=aux_codes[b][:, d_cols].bitcast(FP8X4),
+                        lhsT_scale=aux_scales[b][:, d_cols],
+                        rhs=at_codes[b][:, t_cols].bitcast(FP8X4),
+                        rhs_scale=at_scales[b][:, t_cols],
+                        start=True,
+                        stop=True,
+                    )
+                nc.scalar.copy(
+                    out=pooled[q][:, tt * K_PASS : (tt + 1) * K_PASS].rearrange("p (t s) -> p t s", s=PACK),
+                    in_=wa_ps[:].rearrange("p s t -> p t s"),
+                )
+
+        def transpose_target(b):
+            words = tgt_raw[b][:].bitcast(F32)
+            for g in range(G_TGT):
+                tg_grp = grp.tile([P, LT * PACK], BF16, tag="grp", align_bytes=64)
+                tg_words = tg_grp[:].bitcast(F32)
+                for h in range(T_TILES // 2):
+                    tg_ps = psum_tr.tile([P, 2, 2 * P], F32, tag="tr")
+                    for u in range(2):
+                        for v in range(2):
+                            first = (2 * h + v) * (DT // 2) + (2 * g + u) * P
+                            nc.tensor.transpose(
+                                tg_ps[:, u, v * P : (v + 1) * P], words[:, first : first + P], ident_f32[:]
+                            )
+                    nc.scalar.copy(
+                        out=tg_words[:, h * 4 * P : (h + 1) * 4 * P].rearrange("p (t u) -> p t u", u=2),
+                        in_=tg_ps[:].rearrange("p u t -> p t u"),
+                    )
+                nc.vector.quantize_mx(
+                    out=x_codes[b][:, g, :].bitcast(FP8X4), scales=x_scales[b][:, g, :], in_=tg_grp[:]
+                )
+
+        def quantise_wf_tile(i):
+            wf_grp = grp.tile([P, G_ALL * P * PACK], BF16, tag="grp", align_bytes=64)
+            nc.vector.tensor_copy(
+                out=wf_grp[:].rearrange("p (g c r s) -> p g c s r", g=G_ALL, r=RUN, s=PACK),
+                in_=wf_raw[:, :, :, i * P : (i + 1) * P].rearrange("p g s (c r) -> p g c s r", r=RUN),
+            )
+            nc.vector.quantize_mx(out=wf_codes[:, i, :].bitcast(FP8X4), scales=wf_scales[:, i, :], in_=wf_grp[:])
+
+        def fuse_tile(i, b):
+            acc = psum_acc.tile([P, LT], F32)
+            for g in range(G_ALL):
+                n_cols = slice(g * P, (g + 1) * P)
+                nc.tensor.matmul_mx(
+                    out=acc[:],
+                    lhsT=wf_codes[:, i, n_cols].bitcast(FP8X4),
+                    lhsT_scale=wf_scales[:, i, n_cols],
+                    rhs=x_codes[b][:, g, :].bitcast(FP8X4),
+                    rhs_scale=x_scales[b][:, g, :],
+                    start=(g == 0),
+                    stop=(g == G_ALL - 1),
+                )
+            y = result.tile([P, LT], F32)
+            nc.scalar.activation(out=y[:], in_=acc[:], func=ACT.Tanh, bias=bias_col[:, i : i + 1], scale=1.0)
+            nc.sync.dma_start(out=out[b, i * P : (i + 1) * P, :], in_=y[:])
+
+        for b in range(B):
+            for tt in range(T_TILES):
+                attention_tile(b, tt)
+            quantise_auxiliary(b)
+            pooled = [pooled_grp.tile([P, LT * PACK], BF16, name="pooled", align_bytes=64) for q in range(G_AUX)]
+            for tt in range(T_TILES):
+                pool_tile(b, tt, pooled)
+            for q in range(G_AUX):
+                g = G_TGT + q
+                nc.vector.quantize_mx(
+                    out=x_codes[b][:, g, :].bitcast(FP8X4), scales=x_scales[b][:, g, :], in_=pooled[q][:]
+                )
+        for b in range(B):
+            transpose_target(b)
+
+        for i in range(N_TILES):
+            quantise_wf_tile(i)
+            for b in range(B):
+                fuse_tile(i, b)

@@ -28,6 +28,8 @@ G_ALL = F // K_PASS
 G_TGT = DT // K_PASS
 G_AUX = DA // K_PASS
 RUN = 4
+FOLDS = 3
+WF_AHEAD = 2
 
 FLOPS = 2 * B * LT * LA * DA + 2 * B * LT * F * DT
 
@@ -38,14 +40,15 @@ def tile_informationfusion_pb_kernel(tc, scores, auxiliary, target, Wf, b_f, out
         const = ctx.enter_context(tc.tile_pool(name="const", bufs=1))
         raw = ctx.enter_context(tc.tile_pool(name="raw", bufs=1))
         keep = ctx.enter_context(tc.tile_pool(name="keep", bufs=1))
-        soft = ctx.enter_context(tc.tile_pool(name="soft", bufs=4))
-        small_grp = ctx.enter_context(tc.tile_pool(name="small_grp", bufs=3))
+        fold = ctx.enter_context(tc.tile_pool(name="fold", bufs=1))
+        soft = ctx.enter_context(tc.tile_pool(name="soft", bufs=T_TILES))
         grp = ctx.enter_context(tc.tile_pool(name="grp", bufs=3))
         pooled_grp = ctx.enter_context(tc.tile_pool(name="pooled_grp", bufs=B * G_AUX))
         result = ctx.enter_context(tc.tile_pool(name="result", bufs=4))
         psum_tr = ctx.enter_context(tc.psum_pool(name="psum_tr", bufs=3))
         psum_pool = ctx.enter_context(tc.psum_pool(name="psum_pool", bufs=2))
         psum_acc = ctx.enter_context(tc.psum_pool(name="psum_acc", bufs=3))
+        ctx.enter_context(tc.manual_schedule())
 
         ident_bf = const.tile([P, P], BF16)
         make_identity(nc, ident_bf[:])
@@ -53,6 +56,9 @@ def tile_informationfusion_pb_kernel(tc, scores, auxiliary, target, Wf, b_f, out
         make_identity(nc, ident_f32[:])
         bias_rows = const.tile([P, P], BF16)
         nc.vector.memset(bias_rows[:], 0.0)
+        warm = const.tile([P, 2], F32)
+        nc.vector.memset(warm[:], 0.0)
+        nc.scalar.activation(out=warm[:, 1:2], in_=warm[:, 0:1], func=ACT.Exp)
 
         sc_raw = []
         aux_raw = []
@@ -63,15 +69,25 @@ def tile_informationfusion_pb_kernel(tc, scores, auxiliary, target, Wf, b_f, out
             tgt_raw.append(raw.tile([P, T_TILES * DT], BF16, name="tgt_raw%d" % b))
         wf_raw = raw.tile([P, G_ALL, PACK, DT], BF16)
 
-        for b in range(B):
+        def load_scores(b):
             nc.sync.dma_start(out=sc_raw[b][:], in_=scores[b].rearrange("(tt p) a -> p tt a", p=P))
+
+        def load_auxiliary(b):
             nc.sync.dma_start(out=aux_raw[b][:], in_=auxiliary[b].rearrange("(s p) d -> p s d", p=P))
-        nc.sync.dma_start(out=bias_rows[0:N_TILES, :], in_=b_f.rearrange("(i c) -> i c", c=P))
-        for b in range(B):
+
+        def load_target(b):
             nc.sync.dma_start(
                 out=tgt_raw[b][:].rearrange("p (tt k) -> p tt k", k=DT),
                 in_=target[b].rearrange("(tt p) k -> p tt k", p=P),
             )
+
+        nc.sync.dma_start(out=bias_rows[0:N_TILES, :], in_=b_f.rearrange("(i c) -> i c", c=P))
+        load_scores(0)
+        load_auxiliary(0)
+        load_scores(1)
+        load_target(0)
+        load_auxiliary(1)
+        load_target(1)
         for g in range(G_ALL):
             rows = Wf[g * K_PASS : (g + 1) * K_PASS, :]
             if g < G_TGT:
@@ -96,34 +112,60 @@ def tile_informationfusion_pb_kernel(tc, scores, auxiliary, target, Wf, b_f, out
         neg_max = const.tile([P, B * T_TILES], F32)
         row_sum = const.tile([P, B * T_TILES], F32)
         inv_sum = const.tile([P, B * T_TILES], F32)
-
-        bias_ps = psum_tr.tile([P, P], BF16, tag="tr")
-        nc.tensor.transpose(bias_ps[:], bias_rows[:], ident_bf[:])
         bias_col = const.tile([P, N_TILES], F32)
-        nc.vector.tensor_copy(out=bias_col[:], in_=bias_ps[:, 0:N_TILES])
 
-        def attention_tile(b, tt):
-            col = slice(b * T_TILES + tt, b * T_TILES + tt + 1)
-            t_cols = slice(tt * P, (tt + 1) * P)
-            rows = sc_raw[b][:, tt, :]
-            nc.vector.tensor_reduce(out=neg_max[:, col], in_=rows, axis=AXIS.X, op=ALU.max, negate=True)
-            e = soft.tile([P, LA], F32)
-            nc.scalar.activation(
-                out=e[:], in_=rows, func=ACT.Exp, bias=neg_max[:, col], scale=1.0, accum_out=row_sum[:, col]
-            )
-            nc.vector.reciprocal(out=inv_sum[:, col], in_=row_sum[:, col])
-            attn = soft.tile([P, LA], BF16)
-            nc.vector.tensor_scalar(out=attn[:], in0=e[:], scalar1=inv_sum[:, col], scalar2=None, op0=ALU.mult)
-            at_ps = psum_tr.tile([P, PACK, P], BF16, tag="tr")
-            for s in range(PACK):
-                nc.tensor.transpose(at_ps[:, s, :], attn[:, s * P : (s + 1) * P], ident_bf[:])
-            at_grp = small_grp.tile([P, P * PACK], BF16, align_bytes=64)
-            nc.scalar.copy(
-                out=at_grp[:].rearrange("p (t s) -> p t s", s=PACK), in_=at_ps[:].rearrange("p s t -> p t s")
-            )
-            nc.vector.quantize_mx(
-                out=at_codes[b][:, t_cols].bitcast(FP8X4), scales=at_scales[b][:, t_cols], in_=at_grp[:]
-            )
+        def spread_bias():
+            bias_ps = psum_acc.tile([P, P], BF16, tag="acc")
+            nc.tensor.transpose(bias_ps[:], bias_rows[:], ident_bf[:])
+            nc.vector.tensor_copy(out=bias_col[:], in_=bias_ps[:, 0:N_TILES])
+
+        def row_max(b):
+            src = sc_raw[b]
+            for k in range(FOLDS):
+                width = LA >> (k + 1)
+                dst = fold.tile([P, T_TILES, width], BF16, name="fold%d" % width)
+                nc.vector.tensor_tensor(
+                    out=dst[:], in0=src[:, :, 0:width], in1=src[:, :, width : 2 * width], op=ALU.max
+                )
+                src = dst
+            cols = slice(b * T_TILES, (b + 1) * T_TILES)
+            nc.vector.tensor_reduce(out=neg_max[:, cols], in_=src[:], axis=AXIS.X, op=ALU.max, negate=True)
+
+        def softmax(b):
+            banks = []
+            for tt in range(T_TILES):
+                col = slice(b * T_TILES + tt, b * T_TILES + tt + 1)
+                e = soft.tile([P, LA], F32)
+                nc.scalar.activation(
+                    out=e[:],
+                    in_=sc_raw[b][:, tt, :],
+                    func=ACT.Exp,
+                    bias=neg_max[:, col],
+                    scale=1.0,
+                    accum_out=row_sum[:, col],
+                )
+                nc.vector.reciprocal(out=inv_sum[:, col], in_=row_sum[:, col])
+                attn = soft.tile([P, LA], BF16)
+                nc.vector.tensor_scalar(
+                    out=attn[:], in0=e[:], scalar1=inv_sum[:, col], scalar2=None, op0=ALU.mult
+                )
+                at_ps = psum_tr.tile([P, PACK, P], BF16, tag="tr")
+                for s in range(PACK):
+                    nc.tensor.transpose(at_ps[:, s, :], attn[:, s * P : (s + 1) * P], ident_bf[:])
+                banks.append(at_ps)
+            return banks
+
+        def quantise_attention(b, banks):
+            for tt in range(T_TILES):
+                t_cols = slice(tt * P, (tt + 1) * P)
+                at_grp = soft.tile([P, P * PACK], BF16, align_bytes=64)
+                nc.scalar.copy(
+                    out=at_grp[:].rearrange("p (t s) -> p t s", s=PACK),
+                    in_=banks[tt][:].rearrange("p s t -> p t s"),
+                )
+                nc.vector.quantize_mx(
+                    out=at_codes[b][:, t_cols].bitcast(FP8X4), scales=at_scales[b][:, t_cols], in_=at_grp[:]
+                )
 
         def quantise_auxiliary(b):
             half = DA // 2
@@ -138,24 +180,31 @@ def tile_informationfusion_pb_kernel(tc, scores, auxiliary, target, Wf, b_f, out
                     out=aux_codes[b][:, d_cols].bitcast(FP8X4), scales=aux_scales[b][:, d_cols], in_=aux_grp[:]
                 )
 
-        def pool_tile(b, tt, pooled):
-            t_cols = slice(tt * P, (tt + 1) * P)
-            for q in range(G_AUX):
-                wa_ps = psum_pool.tile([P, PACK, P], F32)
-                for s in range(PACK):
-                    d_cols = slice((q * PACK + s) * P, (q * PACK + s + 1) * P)
-                    nc.tensor.matmul_mx(
-                        out=wa_ps[:, s, :],
-                        lhsT=aux_codes[b][:, d_cols].bitcast(FP8X4),
-                        lhsT_scale=aux_scales[b][:, d_cols],
-                        rhs=at_codes[b][:, t_cols].bitcast(FP8X4),
-                        rhs_scale=at_scales[b][:, t_cols],
-                        start=True,
-                        stop=True,
+        def pool(b):
+            pooled = [pooled_grp.tile([P, LT * PACK], BF16, name="pooled", align_bytes=64) for q in range(G_AUX)]
+            for tt in range(T_TILES):
+                t_cols = slice(tt * P, (tt + 1) * P)
+                for q in range(G_AUX):
+                    wa_ps = psum_pool.tile([P, PACK, P], F32)
+                    for s in range(PACK):
+                        d_cols = slice((q * PACK + s) * P, (q * PACK + s + 1) * P)
+                        nc.tensor.matmul_mx(
+                            out=wa_ps[:, s, :],
+                            lhsT=aux_codes[b][:, d_cols].bitcast(FP8X4),
+                            lhsT_scale=aux_scales[b][:, d_cols],
+                            rhs=at_codes[b][:, t_cols].bitcast(FP8X4),
+                            rhs_scale=at_scales[b][:, t_cols],
+                            start=True,
+                            stop=True,
+                        )
+                    nc.scalar.copy(
+                        out=pooled[q][:, tt * K_PASS : (tt + 1) * K_PASS].rearrange("p (t s) -> p t s", s=PACK),
+                        in_=wa_ps[:].rearrange("p s t -> p t s"),
                     )
-                nc.scalar.copy(
-                    out=pooled[q][:, tt * K_PASS : (tt + 1) * K_PASS].rearrange("p (t s) -> p t s", s=PACK),
-                    in_=wa_ps[:].rearrange("p s t -> p t s"),
+            for q in range(G_AUX):
+                g = G_TGT + q
+                nc.vector.quantize_mx(
+                    out=x_codes[b][:, g, :].bitcast(FP8X4), scales=x_scales[b][:, g, :], in_=pooled[q][:]
                 )
 
         def transpose_target(b):
@@ -188,7 +237,7 @@ def tile_informationfusion_pb_kernel(tc, scores, auxiliary, target, Wf, b_f, out
             nc.vector.quantize_mx(out=wf_codes[:, i, :].bitcast(FP8X4), scales=wf_scales[:, i, :], in_=wf_grp[:])
 
         def fuse_tile(i, b):
-            acc = psum_acc.tile([P, LT], F32)
+            acc = psum_acc.tile([P, LT], F32, tag="acc")
             for g in range(G_ALL):
                 n_cols = slice(g * P, (g + 1) * P)
                 nc.tensor.matmul_mx(
@@ -204,22 +253,25 @@ def tile_informationfusion_pb_kernel(tc, scores, auxiliary, target, Wf, b_f, out
             nc.scalar.activation(out=y[:], in_=acc[:], func=ACT.Tanh, bias=bias_col[:, i : i + 1], scale=1.0)
             nc.sync.dma_start(out=out[b, i * P : (i + 1) * P, :], in_=y[:])
 
+        row_max(0)
+        banks = softmax(0)
+        quantise_auxiliary(0)
+        spread_bias()
         for b in range(B):
-            for tt in range(T_TILES):
-                attention_tile(b, tt)
-            quantise_auxiliary(b)
-            pooled = [pooled_grp.tile([P, LT * PACK], BF16, name="pooled", align_bytes=64) for q in range(G_AUX)]
-            for tt in range(T_TILES):
-                pool_tile(b, tt, pooled)
-            for q in range(G_AUX):
-                g = G_TGT + q
-                nc.vector.quantize_mx(
-                    out=x_codes[b][:, g, :].bitcast(FP8X4), scales=x_scales[b][:, g, :], in_=pooled[q][:]
-                )
-        for b in range(B):
+            quantise_attention(b, banks)
             transpose_target(b)
+            if b + 1 < B:
+                row_max(b + 1)
+                quantise_auxiliary(b + 1)
+            else:
+                for i in range(WF_AHEAD):
+                    quantise_wf_tile(i)
+            pool(b)
+            if b + 1 < B:
+                banks = softmax(b + 1)
 
         for i in range(N_TILES):
-            quantise_wf_tile(i)
+            if i >= WF_AHEAD:
+                quantise_wf_tile(i)
             for b in range(B):
                 fuse_tile(i, b)

@@ -29,7 +29,8 @@ G_TGT = DT // K_PASS
 G_AUX = DA // K_PASS
 RUN = 4
 FOLDS = 3
-WF_AHEAD = 2
+WF_AHEAD = 3
+PSUM_BANKS = 8
 
 FLOPS = 2 * B * LT * LA * DA + 2 * B * LT * F * DT
 
@@ -42,12 +43,10 @@ def tile_informationfusion_pb_kernel(tc, scores, auxiliary, target, Wf, b_f, out
         keep = ctx.enter_context(tc.tile_pool(name="keep", bufs=1))
         fold = ctx.enter_context(tc.tile_pool(name="fold", bufs=1))
         soft = ctx.enter_context(tc.tile_pool(name="soft", bufs=T_TILES))
-        grp = ctx.enter_context(tc.tile_pool(name="grp", bufs=3))
+        grp = ctx.enter_context(tc.tile_pool(name="grp", bufs=4))
         pooled_grp = ctx.enter_context(tc.tile_pool(name="pooled_grp", bufs=B * G_AUX))
         result = ctx.enter_context(tc.tile_pool(name="result", bufs=4))
-        psum_tr = ctx.enter_context(tc.psum_pool(name="psum_tr", bufs=3))
-        psum_pool = ctx.enter_context(tc.psum_pool(name="psum_pool", bufs=2))
-        psum_acc = ctx.enter_context(tc.psum_pool(name="psum_acc", bufs=3))
+        psum = ctx.enter_context(tc.psum_pool(name="psum", bufs=PSUM_BANKS))
         ctx.enter_context(tc.manual_schedule())
 
         ident_bf = const.tile([P, P], BF16)
@@ -81,9 +80,9 @@ def tile_informationfusion_pb_kernel(tc, scores, auxiliary, target, Wf, b_f, out
                 in_=target[b].rearrange("(tt p) k -> p tt k", p=P),
             )
 
-        nc.sync.dma_start(out=bias_rows[0:N_TILES, :], in_=b_f.rearrange("(i c) -> i c", c=P))
         load_scores(0)
         load_auxiliary(0)
+        nc.sync.dma_start(out=bias_rows[0:N_TILES, :], in_=b_f.rearrange("(i c) -> i c", c=P))
         load_scores(1)
         load_target(0)
         load_auxiliary(1)
@@ -115,7 +114,7 @@ def tile_informationfusion_pb_kernel(tc, scores, auxiliary, target, Wf, b_f, out
         bias_col = const.tile([P, N_TILES], F32)
 
         def spread_bias():
-            bias_ps = psum_acc.tile([P, P], BF16, tag="acc")
+            bias_ps = psum.tile([P, P], BF16, tag="bank")
             nc.tensor.transpose(bias_ps[:], bias_rows[:], ident_bf[:])
             nc.vector.tensor_copy(out=bias_col[:], in_=bias_ps[:, 0:N_TILES])
 
@@ -149,7 +148,7 @@ def tile_informationfusion_pb_kernel(tc, scores, auxiliary, target, Wf, b_f, out
                 nc.vector.tensor_scalar(
                     out=attn[:], in0=e[:], scalar1=inv_sum[:, col], scalar2=None, op0=ALU.mult
                 )
-                at_ps = psum_tr.tile([P, PACK, P], BF16, tag="tr")
+                at_ps = psum.tile([P, PACK, P], BF16, tag="bank")
                 for s in range(PACK):
                     nc.tensor.transpose(at_ps[:, s, :], attn[:, s * P : (s + 1) * P], ident_bf[:])
                 banks.append(at_ps)
@@ -167,25 +166,24 @@ def tile_informationfusion_pb_kernel(tc, scores, auxiliary, target, Wf, b_f, out
                     out=at_codes[b][:, t_cols].bitcast(FP8X4), scales=at_scales[b][:, t_cols], in_=at_grp[:]
                 )
 
-        def quantise_auxiliary(b):
-            half = DA // 2
-            for h in range(2):
-                d_cols = slice(h * half, (h + 1) * half)
-                aux_grp = grp.tile([P, half * PACK], BF16, tag="grp", align_bytes=64)
-                nc.vector.tensor_copy(
-                    out=aux_grp[:].rearrange("p (c r s) -> p c s r", r=RUN, s=PACK),
-                    in_=aux_raw[b][:, :, d_cols].rearrange("p s (c r) -> p c s r", r=RUN),
-                )
-                nc.vector.quantize_mx(
-                    out=aux_codes[b][:, d_cols].bitcast(FP8X4), scales=aux_scales[b][:, d_cols], in_=aux_grp[:]
-                )
+        def quantise_auxiliary(b, q):
+            d_cols = slice(q * K_PASS, (q + 1) * K_PASS)
+            aux_grp = grp.tile([P, K_PASS * PACK], BF16, tag="grp", align_bytes=64)
+            nc.vector.tensor_copy(
+                out=aux_grp[:].rearrange("p (c r s) -> p c s r", r=RUN, s=PACK),
+                in_=aux_raw[b][:, :, d_cols].rearrange("p s (c r) -> p c s r", r=RUN),
+            )
+            nc.vector.quantize_mx(
+                out=aux_codes[b][:, d_cols].bitcast(FP8X4), scales=aux_scales[b][:, d_cols], in_=aux_grp[:]
+            )
 
         def pool(b):
-            pooled = [pooled_grp.tile([P, LT * PACK], BF16, name="pooled", align_bytes=64) for q in range(G_AUX)]
-            for tt in range(T_TILES):
-                t_cols = slice(tt * P, (tt + 1) * P)
-                for q in range(G_AUX):
-                    wa_ps = psum_pool.tile([P, PACK, P], F32)
+            pooled = []
+            for q in range(G_AUX):
+                pooled.append(pooled_grp.tile([P, LT * PACK], BF16, name="pooled", align_bytes=64))
+                for tt in range(T_TILES):
+                    t_cols = slice(tt * P, (tt + 1) * P)
+                    wa_ps = psum.tile([P, PACK, P], F32, tag="bank")
                     for s in range(PACK):
                         d_cols = slice((q * PACK + s) * P, (q * PACK + s + 1) * P)
                         nc.tensor.matmul_mx(
@@ -201,6 +199,9 @@ def tile_informationfusion_pb_kernel(tc, scores, auxiliary, target, Wf, b_f, out
                         out=pooled[q][:, tt * K_PASS : (tt + 1) * K_PASS].rearrange("p (t s) -> p t s", s=PACK),
                         in_=wa_ps[:].rearrange("p s t -> p t s"),
                     )
+            return pooled
+
+        def quantise_pooled(b, pooled):
             for q in range(G_AUX):
                 g = G_TGT + q
                 nc.vector.quantize_mx(
@@ -213,7 +214,7 @@ def tile_informationfusion_pb_kernel(tc, scores, auxiliary, target, Wf, b_f, out
                 tg_grp = grp.tile([P, LT * PACK], BF16, tag="grp", align_bytes=64)
                 tg_words = tg_grp[:].bitcast(F32)
                 for h in range(T_TILES // 2):
-                    tg_ps = psum_tr.tile([P, 2, 2 * P], F32, tag="tr")
+                    tg_ps = psum.tile([P, 2, 2 * P], F32, tag="bank")
                     for u in range(2):
                         for v in range(2):
                             first = (2 * h + v) * (DT // 2) + (2 * g + u) * P
@@ -237,7 +238,7 @@ def tile_informationfusion_pb_kernel(tc, scores, auxiliary, target, Wf, b_f, out
             nc.vector.quantize_mx(out=wf_codes[:, i, :].bitcast(FP8X4), scales=wf_scales[:, i, :], in_=wf_grp[:])
 
         def fuse_tile(i, b):
-            acc = psum_acc.tile([P, LT], F32, tag="acc")
+            acc = psum.tile([P, LT], F32, tag="bank")
             for g in range(G_ALL):
                 n_cols = slice(g * P, (g + 1) * P)
                 nc.tensor.matmul_mx(
@@ -255,23 +256,30 @@ def tile_informationfusion_pb_kernel(tc, scores, auxiliary, target, Wf, b_f, out
 
         row_max(0)
         banks = softmax(0)
-        quantise_auxiliary(0)
+        quantise_auxiliary(0, 0)
+        quantise_attention(0, banks)
+        quantise_auxiliary(0, 1)
+        transpose_target(0)
         spread_bias()
-        for b in range(B):
-            quantise_attention(b, banks)
-            transpose_target(b)
-            if b + 1 < B:
-                row_max(b + 1)
-                quantise_auxiliary(b + 1)
-            else:
-                for i in range(WF_AHEAD):
-                    quantise_wf_tile(i)
-            pool(b)
-            if b + 1 < B:
-                banks = softmax(b + 1)
+        row_max(1)
+        quantise_auxiliary(1, 0)
+        quantise_auxiliary(1, 1)
+        pooled = pool(0)
+        banks = softmax(1)
+        quantise_pooled(0, pooled)
+        quantise_wf_tile(0)
+        quantise_attention(1, banks)
+        quantise_wf_tile(1)
+        transpose_target(1)
+        for i in range(2, WF_AHEAD):
+            quantise_wf_tile(i)
+        pooled = pool(1)
+        quantise_pooled(1, pooled)
 
-        for i in range(N_TILES):
-            if i >= WF_AHEAD:
-                quantise_wf_tile(i)
+        for b in range(B):
+            for i in range(WF_AHEAD):
+                fuse_tile(i, b)
+        for i in range(WF_AHEAD, N_TILES):
+            quantise_wf_tile(i)
             for b in range(B):
                 fuse_tile(i, b)

@@ -28,7 +28,6 @@ G_ALL = F // K_PASS
 G_TGT = DT // K_PASS
 G_AUX = DA // K_PASS
 RUN = 4
-FOLDS = 3
 WF_AHEAD = 3
 PSUM_BANKS = 8
 
@@ -41,11 +40,10 @@ def tile_informationfusion_pb_kernel(tc, scores, auxiliary, target, Wf, b_f, out
         const = ctx.enter_context(tc.tile_pool(name="const", bufs=1))
         raw = ctx.enter_context(tc.tile_pool(name="raw", bufs=1))
         keep = ctx.enter_context(tc.tile_pool(name="keep", bufs=1))
-        fold = ctx.enter_context(tc.tile_pool(name="fold", bufs=1))
         soft = ctx.enter_context(tc.tile_pool(name="soft", bufs=T_TILES))
         grp = ctx.enter_context(tc.tile_pool(name="grp", bufs=4))
         pooled_grp = ctx.enter_context(tc.tile_pool(name="pooled_grp", bufs=B * G_AUX))
-        result = ctx.enter_context(tc.tile_pool(name="result", bufs=4))
+        result = ctx.enter_context(tc.tile_pool(name="result", bufs=8))
         psum = ctx.enter_context(tc.psum_pool(name="psum", bufs=PSUM_BANKS))
         ctx.enter_context(tc.manual_schedule())
 
@@ -69,7 +67,8 @@ def tile_informationfusion_pb_kernel(tc, scores, auxiliary, target, Wf, b_f, out
         wf_raw = raw.tile([P, G_ALL, PACK, DT], BF16)
 
         def load_scores(b):
-            nc.sync.dma_start(out=sc_raw[b][:], in_=scores[b].rearrange("(tt p) a -> p tt a", p=P))
+            for tt in range(T_TILES):
+                nc.sync.dma_start(out=sc_raw[b][:, tt, :], in_=scores[b, tt * P : (tt + 1) * P, :])
 
         def load_auxiliary(b):
             nc.sync.dma_start(out=aux_raw[b][:], in_=auxiliary[b].rearrange("(s p) d -> p s d", p=P))
@@ -83,8 +82,8 @@ def tile_informationfusion_pb_kernel(tc, scores, auxiliary, target, Wf, b_f, out
         load_scores(0)
         load_auxiliary(0)
         nc.sync.dma_start(out=bias_rows[0:N_TILES, :], in_=b_f.rearrange("(i c) -> i c", c=P))
-        load_scores(1)
         load_target(0)
+        load_scores(1)
         load_auxiliary(1)
         load_target(1)
         for g in range(G_ALL):
@@ -119,16 +118,11 @@ def tile_informationfusion_pb_kernel(tc, scores, auxiliary, target, Wf, b_f, out
             nc.vector.tensor_copy(out=bias_col[:], in_=bias_ps[:, 0:N_TILES])
 
         def row_max(b):
-            src = sc_raw[b]
-            for k in range(FOLDS):
-                width = LA >> (k + 1)
-                dst = fold.tile([P, T_TILES, width], BF16, name="fold%d" % width)
-                nc.vector.tensor_tensor(
-                    out=dst[:], in0=src[:, :, 0:width], in1=src[:, :, width : 2 * width], op=ALU.max
+            for tt in range(T_TILES):
+                col = slice(b * T_TILES + tt, b * T_TILES + tt + 1)
+                nc.vector.tensor_reduce(
+                    out=neg_max[:, col], in_=sc_raw[b][:, tt, :], axis=AXIS.X, op=ALU.max, negate=True
                 )
-                src = dst
-            cols = slice(b * T_TILES, (b + 1) * T_TILES)
-            nc.vector.tensor_reduce(out=neg_max[:, cols], in_=src[:], axis=AXIS.X, op=ALU.max, negate=True)
 
         def softmax(b):
             banks = []

@@ -85,7 +85,6 @@ def tile_informationfusion_pb_kernel(tc, scores, auxiliary, target, Wf, b_f, out
         load_target(0)
         load_scores(1)
         load_auxiliary(1)
-        load_target(1)
         for g in range(G_ALL):
             rows = Wf[g * K_PASS : (g + 1) * K_PASS, :]
             if g < G_TGT:
@@ -95,6 +94,7 @@ def tile_informationfusion_pb_kernel(tc, scores, auxiliary, target, Wf, b_f, out
                 )
             else:
                 nc.sync.dma_start(out=wf_raw[:, g, :, :], in_=rows.rearrange("(s p) n -> p s n", p=P))
+        load_target(1)
 
         at_codes, at_scales, aux_codes, aux_scales, x_codes, x_scales = [], [], [], [], [], []
         for b in range(B):

@@ -41,7 +41,7 @@ def tile_informationfusion_pb_kernel(tc, scores, auxiliary, target, Wf, b_f, out
         raw = ctx.enter_context(tc.tile_pool(name="raw", bufs=1))
         keep = ctx.enter_context(tc.tile_pool(name="keep", bufs=1))
         soft = ctx.enter_context(tc.tile_pool(name="soft", bufs=T_TILES))
-        grp = ctx.enter_context(tc.tile_pool(name="grp", bufs=4))
+        grp = ctx.enter_context(tc.tile_pool(name="grp", bufs=6))
         pooled_grp = ctx.enter_context(tc.tile_pool(name="pooled_grp", bufs=B * G_AUX))
         result = ctx.enter_context(tc.tile_pool(name="result", bufs=8))
         psum = ctx.enter_context(tc.psum_pool(name="psum", bufs=PSUM_BANKS))
@@ -160,13 +160,17 @@ def tile_informationfusion_pb_kernel(tc, scores, auxiliary, target, Wf, b_f, out
                     out=at_codes[b][:, t_cols].bitcast(FP8X4), scales=at_scales[b][:, t_cols], in_=at_grp[:]
                 )
 
-        def quantise_auxiliary(b, q):
+        def regroup_auxiliary(b, q):
             d_cols = slice(q * K_PASS, (q + 1) * K_PASS)
             aux_grp = grp.tile([P, K_PASS * PACK], BF16, tag="grp", align_bytes=64)
             nc.vector.tensor_copy(
                 out=aux_grp[:].rearrange("p (c r s) -> p c s r", r=RUN, s=PACK),
                 in_=aux_raw[b][:, :, d_cols].rearrange("p s (c r) -> p c s r", r=RUN),
             )
+            return aux_grp
+
+        def quantise_auxiliary(b, q, aux_grp):
+            d_cols = slice(q * K_PASS, (q + 1) * K_PASS)
             nc.vector.quantize_mx(
                 out=aux_codes[b][:, d_cols].bitcast(FP8X4), scales=aux_scales[b][:, d_cols], in_=aux_grp[:]
             )
@@ -223,12 +227,15 @@ def tile_informationfusion_pb_kernel(tc, scores, auxiliary, target, Wf, b_f, out
                     out=x_codes[b][:, g, :].bitcast(FP8X4), scales=x_scales[b][:, g, :], in_=tg_grp[:]
                 )
 
-        def quantise_wf_tile(i):
+        def regroup_wf_tile(i):
             wf_grp = grp.tile([P, G_ALL * P * PACK], BF16, tag="grp", align_bytes=64)
             nc.vector.tensor_copy(
                 out=wf_grp[:].rearrange("p (g c r s) -> p g c s r", g=G_ALL, r=RUN, s=PACK),
                 in_=wf_raw[:, :, :, i * P : (i + 1) * P].rearrange("p g s (c r) -> p g c s r", r=RUN),
             )
+            return wf_grp
+
+        def quantise_wf_tile(i, wf_grp):
             nc.vector.quantize_mx(out=wf_codes[:, i, :].bitcast(FP8X4), scales=wf_scales[:, i, :], in_=wf_grp[:])
 
         def fuse_tile(i, b):
@@ -250,23 +257,30 @@ def tile_informationfusion_pb_kernel(tc, scores, auxiliary, target, Wf, b_f, out
 
         row_max(0)
         banks = softmax(0)
-        quantise_auxiliary(0, 0)
+        aux_0 = regroup_auxiliary(0, 0)
+        aux_1 = regroup_auxiliary(0, 1)
+        quantise_auxiliary(0, 0, aux_0)
         quantise_attention(0, banks)
-        quantise_auxiliary(0, 1)
+        quantise_auxiliary(0, 1, aux_1)
         transpose_target(0)
         spread_bias()
         row_max(1)
-        quantise_auxiliary(1, 0)
-        quantise_auxiliary(1, 1)
+        aux_0 = regroup_auxiliary(1, 0)
+        aux_1 = regroup_auxiliary(1, 1)
+        quantise_auxiliary(1, 0, aux_0)
+        quantise_auxiliary(1, 1, aux_1)
         pooled = pool(0)
         banks = softmax(1)
+        wf_grp = [regroup_wf_tile(0)]
         quantise_pooled(0, pooled)
-        quantise_wf_tile(0)
+        quantise_wf_tile(0, wf_grp[0])
+        wf_grp.append(regroup_wf_tile(1))
         quantise_attention(1, banks)
-        quantise_wf_tile(1)
+        quantise_wf_tile(1, wf_grp[1])
+        wf_grp.append(regroup_wf_tile(2))
         transpose_target(1)
-        for i in range(2, WF_AHEAD):
-            quantise_wf_tile(i)
+        quantise_wf_tile(2, wf_grp[2])
+        wf_grp.append(regroup_wf_tile(3))
         pooled = pool(1)
         quantise_pooled(1, pooled)
 
@@ -274,6 +288,8 @@ def tile_informationfusion_pb_kernel(tc, scores, auxiliary, target, Wf, b_f, out
             for i in range(WF_AHEAD):
                 fuse_tile(i, b)
         for i in range(WF_AHEAD, N_TILES):
-            quantise_wf_tile(i)
+            if i + 1 < N_TILES:
+                wf_grp.append(regroup_wf_tile(i + 1))
+            quantise_wf_tile(i, wf_grp[i])
             for b in range(B):
                 fuse_tile(i, b)

@@ -28,6 +28,7 @@ G_ALL = F // K_PASS
 G_TGT = DT // K_PASS
 G_AUX = DA // K_PASS
 RUN = 4
+WF_HALF = DT // 2
 WF_AHEAD = 3
 PSUM_BANKS = 8
 
@@ -79,22 +80,26 @@ def tile_informationfusion_pb_kernel(tc, scores, auxiliary, target, Wf, b_f, out
                 in_=target[b].rearrange("(tt p) k -> p tt k", p=P),
             )
 
+        def load_wf(half):
+            n_cols = slice(half * WF_HALF, (half + 1) * WF_HALF)
+            for g in range(G_ALL):
+                rows = Wf[g * K_PASS : (g + 1) * K_PASS, n_cols]
+                if g < G_TGT:
+                    pairs = rows.rearrange("(u p e) n -> p u e n", p=P, e=2)
+                    for u in range(2):
+                        nc.sync.dma_start(out=wf_raw[:, g, 2 * u : 2 * u + 2, n_cols], in_=pairs[:, u, :, :])
+                else:
+                    nc.sync.dma_start(out=wf_raw[:, g, :, n_cols], in_=rows.rearrange("(s p) n -> p s n", p=P))
+
         load_scores(0)
         load_auxiliary(0)
         nc.sync.dma_start(out=bias_rows[0:N_TILES, :], in_=b_f.rearrange("(i c) -> i c", c=P))
         load_target(0)
         load_scores(1)
         load_auxiliary(1)
-        for g in range(G_ALL):
-            rows = Wf[g * K_PASS : (g + 1) * K_PASS, :]
-            if g < G_TGT:
-                nc.sync.dma_start(
-                    out=wf_raw[:, g, :, :].rearrange("p (u e) n -> p u (e n)", e=2),
-                    in_=rows.rearrange("(u p e) n -> p u (e n)", p=P, e=2),
-                )
-            else:
-                nc.sync.dma_start(out=wf_raw[:, g, :, :], in_=rows.rearrange("(s p) n -> p s n", p=P))
+        load_wf(0)
         load_target(1)
+        load_wf(1)
 
         at_codes, at_scales, aux_codes, aux_scales, x_codes, x_scales = [], [], [], [], [], []
         for b in range(B):

@@ -30,6 +30,7 @@ G_AUX = DA // K_PASS
 RUN = 4
 WF_HALF = DT // 2
 WF_AHEAD = 3
+HALVINGS = 3
 PSUM_BANKS = 8
 
 FLOPS = 2 * B * LT * LA * DA + 2 * B * LT * F * DT
@@ -42,7 +43,7 @@ def tile_informationfusion_pb_kernel(tc, scores, auxiliary, target, Wf, b_f, out
         raw = ctx.enter_context(tc.tile_pool(name="raw", bufs=1))
         keep = ctx.enter_context(tc.tile_pool(name="keep", bufs=1))
         soft = ctx.enter_context(tc.tile_pool(name="soft", bufs=T_TILES))
-        grp = ctx.enter_context(tc.tile_pool(name="grp", bufs=6))
+        grp = ctx.enter_context(tc.tile_pool(name="grp", bufs=4))
         pooled_grp = ctx.enter_context(tc.tile_pool(name="pooled_grp", bufs=B * G_AUX))
         result = ctx.enter_context(tc.tile_pool(name="result", bufs=8))
         psum = ctx.enter_context(tc.psum_pool(name="psum", bufs=PSUM_BANKS))
@@ -65,20 +66,13 @@ def tile_informationfusion_pb_kernel(tc, scores, auxiliary, target, Wf, b_f, out
             sc_raw.append(raw.tile([P, T_TILES, LA], BF16, name="sc_raw%d" % b))
             aux_raw.append(raw.tile([P, PACK, DA], BF16, name="aux_raw%d" % b))
             tgt_raw.append(raw.tile([P, T_TILES * DT], BF16, name="tgt_raw%d" % b))
-        wf_raw = raw.tile([P, G_ALL, PACK, DT], BF16)
-
-        def load_scores(b):
-            for tt in range(T_TILES):
-                nc.sync.dma_start(out=sc_raw[b][:, tt, :], in_=scores[b, tt * P : (tt + 1) * P, :])
+        wf_raw = [raw.tile([P, G_ALL, PACK, WF_HALF], BF16, name="wf_raw%d" % h) for h in range(2)]
 
         def load_auxiliary(b):
             nc.sync.dma_start(out=aux_raw[b][:], in_=auxiliary[b].rearrange("(s p) d -> p s d", p=P))
 
         def load_target(b):
-            nc.sync.dma_start(
-                out=tgt_raw[b][:].rearrange("p (tt k) -> p tt k", k=DT),
-                in_=target[b].rearrange("(tt p) k -> p tt k", p=P),
-            )
+            nc.sync.dma_start(out=tgt_raw[b][:], in_=target[b].rearrange("(p tt) k -> p (tt k)", tt=T_TILES))
 
         def load_wf(half):
             n_cols = slice(half * WF_HALF, (half + 1) * WF_HALF)
@@ -87,15 +81,17 @@ def tile_informationfusion_pb_kernel(tc, scores, auxiliary, target, Wf, b_f, out
                 if g < G_TGT:
                     pairs = rows.rearrange("(u p e) n -> p u e n", p=P, e=2)
                     for u in range(2):
-                        nc.sync.dma_start(out=wf_raw[:, g, 2 * u : 2 * u + 2, n_cols], in_=pairs[:, u, :, :])
+                        nc.sync.dma_start(out=wf_raw[half][:, g, 2 * u : 2 * u + 2, :], in_=pairs[:, u, :, :])
                 else:
-                    nc.sync.dma_start(out=wf_raw[:, g, :, n_cols], in_=rows.rearrange("(s p) n -> p s n", p=P))
+                    nc.sync.dma_start(out=wf_raw[half][:, g, :, :], in_=rows.rearrange("(s p) n -> p s n", p=P))
 
-        load_scores(0)
+        by_partition = [scores[b].rearrange("(p tt) a -> p tt a", tt=T_TILES) for b in range(B)]
+        for tt in range(T_TILES):
+            nc.sync.dma_start(out=sc_raw[0][:, tt, :], in_=by_partition[0][:, tt, :])
         load_auxiliary(0)
         nc.sync.dma_start(out=bias_rows[0:N_TILES, :], in_=b_f.rearrange("(i c) -> i c", c=P))
         load_target(0)
-        load_scores(1)
+        nc.sync.dma_start(out=sc_raw[1][:], in_=by_partition[1])
         load_auxiliary(1)
         load_wf(0)
         load_target(1)
@@ -116,59 +112,76 @@ def tile_informationfusion_pb_kernel(tc, scores, auxiliary, target, Wf, b_f, out
         row_sum = const.tile([P, B * T_TILES], F32)
         inv_sum = const.tile([P, B * T_TILES], F32)
         bias_col = const.tile([P, N_TILES], F32)
+        halved = [const.tile([P, T_TILES, LA >> (j + 1)], BF16, name="halved%d" % j) for j in range(HALVINGS)]
 
-        def spread_bias():
+        def stat(b, tt):
+            return slice(b * T_TILES + tt, b * T_TILES + tt + 1)
+
+        def transpose_bias():
             bias_ps = psum.tile([P, P], BF16, tag="bank")
             nc.tensor.transpose(bias_ps[:], bias_rows[:], ident_bf[:])
-            nc.vector.tensor_copy(out=bias_col[:], in_=bias_ps[:, 0:N_TILES])
+            return bias_ps
 
-        def row_max(b):
-            for tt in range(T_TILES):
-                col = slice(b * T_TILES + tt, b * T_TILES + tt + 1)
-                nc.vector.tensor_reduce(
-                    out=neg_max[:, col], in_=sc_raw[b][:, tt, :], axis=AXIS.X, op=ALU.max, negate=True
-                )
+        def row_max(b, tt):
+            nc.vector.tensor_reduce(
+                out=neg_max[:, stat(b, tt)], in_=sc_raw[b][:, tt, :], axis=AXIS.X, op=ALU.max, negate=True
+            )
 
-        def softmax(b):
-            banks = []
-            for tt in range(T_TILES):
-                col = slice(b * T_TILES + tt, b * T_TILES + tt + 1)
-                e = soft.tile([P, LA], F32)
-                nc.scalar.activation(
-                    out=e[:],
-                    in_=sc_raw[b][:, tt, :],
-                    func=ACT.Exp,
-                    bias=neg_max[:, col],
-                    scale=1.0,
-                    accum_out=row_sum[:, col],
-                )
-                nc.vector.reciprocal(out=inv_sum[:, col], in_=row_sum[:, col])
-                attn = soft.tile([P, LA], BF16)
-                nc.vector.tensor_scalar(
-                    out=attn[:], in0=e[:], scalar1=inv_sum[:, col], scalar2=None, op0=ALU.mult
-                )
-                at_ps = psum.tile([P, PACK, P], BF16, tag="bank")
-                for s in range(PACK):
-                    nc.tensor.transpose(at_ps[:, s, :], attn[:, s * P : (s + 1) * P], ident_bf[:])
-                banks.append(at_ps)
-            return banks
+        def halve_rows(b, j):
+            rows = sc_raw[b] if j == 0 else halved[j - 1]
+            width = LA >> (j + 1)
+            nc.vector.tensor_tensor(
+                out=halved[j][:], in0=rows[:, :, 0:width], in1=rows[:, :, width : 2 * width], op=ALU.max
+            )
 
-        def quantise_attention(b, banks):
-            for tt in range(T_TILES):
-                t_cols = slice(tt * P, (tt + 1) * P)
-                at_grp = soft.tile([P, P * PACK], BF16, align_bytes=64)
-                nc.scalar.copy(
-                    out=at_grp[:].rearrange("p (t s) -> p t s", s=PACK),
-                    in_=banks[tt][:].rearrange("p s t -> p t s"),
-                )
-                nc.vector.quantize_mx(
-                    out=at_codes[b][:, t_cols].bitcast(FP8X4), scales=at_scales[b][:, t_cols], in_=at_grp[:]
-                )
+        def row_max_of_halved(b):
+            nc.vector.tensor_reduce(
+                out=neg_max[:, b * T_TILES : (b + 1) * T_TILES],
+                in_=halved[HALVINGS - 1][:],
+                axis=AXIS.X,
+                op=ALU.max,
+                negate=True,
+            )
 
-        def regroup_auxiliary(b, q):
+        def exponentiate(b, tt):
+            e = soft.tile([P, LA], F32, name="e")
+            nc.scalar.activation(
+                out=e[:],
+                in_=sc_raw[b][:, tt, :],
+                func=ACT.Exp,
+                bias=neg_max[:, stat(b, tt)],
+                scale=1.0,
+                accum_out=row_sum[:, stat(b, tt)],
+            )
+            return e
+
+        def normalise(b, tt, e):
+            attn = soft.tile([P, LA], BF16, name="attn")
+            nc.vector.tensor_scalar(
+                out=attn[:], in0=e[:], scalar1=inv_sum[:, stat(b, tt)], scalar2=None, op0=ALU.mult
+            )
+            at_ps = psum.tile([P, PACK, P], BF16, tag="bank", name="at_ps")
+            for s in range(PACK):
+                nc.tensor.transpose(at_ps[:, s, :], attn[:, s * P : (s + 1) * P], ident_bf[:])
+            return at_ps
+
+        def regroup_attention(bank):
+            at_grp = soft.tile([P, P * PACK], BF16, name="at_grp", align_bytes=64)
+            nc.scalar.copy(
+                out=at_grp[:].rearrange("p (t s) -> p t s", s=PACK), in_=bank[:].rearrange("p s t -> p t s")
+            )
+            return at_grp
+
+        def quantise_attention(b, tt, at_grp):
+            t_cols = slice(tt * P, (tt + 1) * P)
+            nc.vector.quantize_mx(
+                out=at_codes[b][:, t_cols].bitcast(FP8X4), scales=at_scales[b][:, t_cols], in_=at_grp[:]
+            )
+
+        def regroup_auxiliary(b, q, copy):
             d_cols = slice(q * K_PASS, (q + 1) * K_PASS)
-            aux_grp = grp.tile([P, K_PASS * PACK], BF16, tag="grp", align_bytes=64)
-            nc.vector.tensor_copy(
+            aux_grp = grp.tile([P, K_PASS * PACK], BF16, name="aux_grp", align_bytes=64)
+            copy(
                 out=aux_grp[:].rearrange("p (c r s) -> p c s r", r=RUN, s=PACK),
                 in_=aux_raw[b][:, :, d_cols].rearrange("p s (c r) -> p c s r", r=RUN),
             )
@@ -180,44 +193,47 @@ def tile_informationfusion_pb_kernel(tc, scores, auxiliary, target, Wf, b_f, out
                 out=aux_codes[b][:, d_cols].bitcast(FP8X4), scales=aux_scales[b][:, d_cols], in_=aux_grp[:]
             )
 
-        def pool(b):
-            pooled = []
-            for q in range(G_AUX):
-                pooled.append(pooled_grp.tile([P, LT * PACK], BF16, name="pooled", align_bytes=64))
-                for tt in range(T_TILES):
-                    t_cols = slice(tt * P, (tt + 1) * P)
-                    wa_ps = psum.tile([P, PACK, P], F32, tag="bank")
-                    for s in range(PACK):
-                        d_cols = slice((q * PACK + s) * P, (q * PACK + s + 1) * P)
-                        nc.tensor.matmul_mx(
-                            out=wa_ps[:, s, :],
-                            lhsT=aux_codes[b][:, d_cols].bitcast(FP8X4),
-                            lhsT_scale=aux_scales[b][:, d_cols],
-                            rhs=at_codes[b][:, t_cols].bitcast(FP8X4),
-                            rhs_scale=at_scales[b][:, t_cols],
-                            start=True,
-                            stop=True,
-                        )
-                    nc.scalar.copy(
-                        out=pooled[q][:, tt * K_PASS : (tt + 1) * K_PASS].rearrange("p (t s) -> p t s", s=PACK),
-                        in_=wa_ps[:].rearrange("p s t -> p t s"),
+        def pool(b, q):
+            banks = []
+            for tt in range(T_TILES):
+                t_cols = slice(tt * P, (tt + 1) * P)
+                wa_ps = psum.tile([P, PACK, P], F32, tag="bank", name="wa_ps")
+                for s in range(PACK):
+                    d_cols = slice((q * PACK + s) * P, (q * PACK + s + 1) * P)
+                    nc.tensor.matmul_mx(
+                        out=wa_ps[:, s, :],
+                        lhsT=aux_codes[b][:, d_cols].bitcast(FP8X4),
+                        lhsT_scale=aux_scales[b][:, d_cols],
+                        rhs=at_codes[b][:, t_cols].bitcast(FP8X4),
+                        rhs_scale=at_scales[b][:, t_cols],
+                        start=True,
+                        stop=True,
                     )
+                banks.append(wa_ps)
+            return banks
+
+        def regroup_pooled(banks):
+            pooled = pooled_grp.tile([P, LT * PACK], BF16, name="pooled", align_bytes=64)
+            for tt in range(T_TILES):
+                nc.scalar.copy(
+                    out=pooled[:, tt * K_PASS : (tt + 1) * K_PASS].rearrange("p (t s) -> p t s", s=PACK),
+                    in_=banks[tt][:].rearrange("p s t -> p t s"),
+                )
             return pooled
 
-        def quantise_pooled(b, pooled):
-            for q in range(G_AUX):
-                g = G_TGT + q
-                nc.vector.quantize_mx(
-                    out=x_codes[b][:, g, :].bitcast(FP8X4), scales=x_scales[b][:, g, :], in_=pooled[q][:]
-                )
+        def quantise_x(b, g, x_grp):
+            nc.vector.quantize_mx(
+                out=x_codes[b][:, g, :].bitcast(FP8X4), scales=x_scales[b][:, g, :], in_=x_grp[:]
+            )
 
         def transpose_target(b):
             words = tgt_raw[b][:].bitcast(F32)
+            groups = []
             for g in range(G_TGT):
-                tg_grp = grp.tile([P, LT * PACK], BF16, tag="grp", align_bytes=64)
+                tg_grp = grp.tile([P, LT * PACK], BF16, name="tg_grp", align_bytes=64)
                 tg_words = tg_grp[:].bitcast(F32)
                 for h in range(T_TILES // 2):
-                    tg_ps = psum.tile([P, 2, 2 * P], F32, tag="bank")
+                    tg_ps = psum.tile([P, 2, 2 * P], F32, tag="bank", name="tg_ps")
                     for u in range(2):
                         for v in range(2):
                             first = (2 * h + v) * (DT // 2) + (2 * g + u) * P
@@ -228,15 +244,15 @@ def tile_informationfusion_pb_kernel(tc, scores, auxiliary, target, Wf, b_f, out
                         out=tg_words[:, h * 4 * P : (h + 1) * 4 * P].rearrange("p (t u) -> p t u", u=2),
                         in_=tg_ps[:].rearrange("p u t -> p t u"),
                     )
-                nc.vector.quantize_mx(
-                    out=x_codes[b][:, g, :].bitcast(FP8X4), scales=x_scales[b][:, g, :], in_=tg_grp[:]
-                )
+                groups.append(tg_grp)
+            return groups
 
-        def regroup_wf_tile(i):
-            wf_grp = grp.tile([P, G_ALL * P * PACK], BF16, tag="grp", align_bytes=64)
-            nc.vector.tensor_copy(
+        def regroup_wf_tile(i, copy):
+            half, first = divmod(i * P, WF_HALF)
+            wf_grp = grp.tile([P, G_ALL * P * PACK], BF16, name="wf_grp", align_bytes=64)
+            copy(
                 out=wf_grp[:].rearrange("p (g c r s) -> p g c s r", g=G_ALL, r=RUN, s=PACK),
-                in_=wf_raw[:, :, :, i * P : (i + 1) * P].rearrange("p g s (c r) -> p g c s r", r=RUN),
+                in_=wf_raw[half][:, :, :, first : first + P].rearrange("p g s (c r) -> p g c s r", r=RUN),
             )
             return wf_grp
 
@@ -257,44 +273,91 @@ def tile_informationfusion_pb_kernel(tc, scores, auxiliary, target, Wf, b_f, out
                     stop=(g == G_ALL - 1),
                 )
             y = result.tile([P, LT], F32)
-            nc.scalar.activation(out=y[:], in_=acc[:], func=ACT.Tanh, bias=bias_col[:, i : i + 1], scale=1.0)
+            nc.scalar.activation(
+                out=y[:].rearrange("n (p tt) -> n p tt", tt=T_TILES),
+                in_=acc[:].rearrange("n (tt p) -> n p tt", tt=T_TILES),
+                func=ACT.Tanh,
+                bias=bias_col[:, i : i + 1],
+                scale=1.0,
+            )
             nc.sync.dma_start(out=out[b, i * P : (i + 1) * P, :], in_=y[:])
 
-        row_max(0)
-        banks = softmax(0)
-        aux_0 = regroup_auxiliary(0, 0)
-        aux_1 = regroup_auxiliary(0, 1)
-        quantise_auxiliary(0, 0, aux_0)
-        quantise_attention(0, banks)
-        quantise_auxiliary(0, 1, aux_1)
-        transpose_target(0)
-        spread_bias()
-        row_max(1)
-        aux_0 = regroup_auxiliary(1, 0)
-        aux_1 = regroup_auxiliary(1, 1)
-        quantise_auxiliary(1, 0, aux_0)
-        quantise_auxiliary(1, 1, aux_1)
-        pooled = pool(0)
-        banks = softmax(1)
-        wf_grp = [regroup_wf_tile(0)]
-        quantise_pooled(0, pooled)
-        quantise_wf_tile(0, wf_grp[0])
-        wf_grp.append(regroup_wf_tile(1))
-        quantise_attention(1, banks)
-        quantise_wf_tile(1, wf_grp[1])
-        wf_grp.append(regroup_wf_tile(2))
-        transpose_target(1)
-        quantise_wf_tile(2, wf_grp[2])
-        wf_grp.append(regroup_wf_tile(3))
-        pooled = pool(1)
-        quantise_pooled(1, pooled)
+        on_vector, on_scalar = nc.vector.tensor_copy, nc.scalar.copy
 
-        for b in range(B):
-            for i in range(WF_AHEAD):
-                fuse_tile(i, b)
+        e, at_ps = {}, {}
+        for j in range(T_TILES + 3):
+            if j < T_TILES:
+                row_max(0, j)
+                e[j] = exponentiate(0, j)
+            if 0 <= j - 2 < T_TILES:
+                nc.vector.reciprocal(out=inv_sum[:, stat(0, j - 2)], in_=row_sum[:, stat(0, j - 2)])
+            if 0 <= j - 3 < T_TILES:
+                at_ps[j - 3] = normalise(0, j - 3, e[j - 3])
+        aux_0 = regroup_auxiliary(0, 0, on_vector)
+        aux_1 = regroup_auxiliary(0, 1, on_scalar)
+        quantise_auxiliary(0, 0, aux_0)
+        at_grp = [regroup_attention(at_ps[tt]) for tt in range(T_TILES)]
+        quantise_auxiliary(0, 1, aux_1)
+        for tt in range(T_TILES):
+            quantise_attention(0, tt, at_grp[tt])
+        target_0 = transpose_target(0)
+        bias_ps = transpose_bias()
+
+        halve_rows(1, 0)
+        halve_rows(1, 1)
+        quantise_x(0, 0, target_0[0])
+        halve_rows(1, 2)
+        nc.vector.tensor_copy(out=bias_col[:], in_=bias_ps[:, 0:N_TILES])
+        row_max_of_halved(1)
+        sums_0 = pool(0, 0)
+        sums_1 = pool(0, 1)
+        e = [exponentiate(1, tt) for tt in range(T_TILES)]
+        pooled_0 = regroup_pooled(sums_0)
+        aux_0 = regroup_auxiliary(1, 0, on_vector)
+        quantise_x(0, 1, target_0[1])
+        aux_1 = regroup_auxiliary(1, 1, on_vector)
+        nc.vector.reciprocal(out=inv_sum[:, T_TILES : 2 * T_TILES], in_=row_sum[:, T_TILES : 2 * T_TILES])
+        quantise_auxiliary(1, 0, aux_0)
+        at_ps = [normalise(1, tt, e[tt]) for tt in range(T_TILES)]
+        quantise_auxiliary(1, 1, aux_1)
+        wf_grp = [regroup_wf_tile(0, on_vector)]
+        at_grp = [regroup_attention(at_ps[tt]) for tt in range(T_TILES)]
+        for tt in range(T_TILES):
+            quantise_attention(1, tt, at_grp[tt])
+        pooled_1 = regroup_pooled(sums_1)
+        wf_grp.append(regroup_wf_tile(1, on_vector))
+        quantise_wf_tile(0, wf_grp[0])
+        quantise_x(0, G_TGT, pooled_0)
+        quantise_x(0, G_TGT + 1, pooled_1)
+        quantise_wf_tile(1, wf_grp[1])
+        target_1 = transpose_target(1)
+        sums_0 = pool(1, 0)
+        pooled_0 = regroup_pooled(sums_0)
+        sums_1 = pool(1, 1)
+        pooled_1 = regroup_pooled(sums_1)
+        wf_grp.append(regroup_wf_tile(2, on_vector))
+        quantise_x(1, 0, target_1[0])
+        quantise_x(1, 1, target_1[1])
+        quantise_wf_tile(2, wf_grp[2])
+        wf_grp.append(regroup_wf_tile(3, on_vector))
+        quantise_x(1, G_TGT, pooled_0)
+        quantise_x(1, G_TGT + 1, pooled_1)
+        quantise_wf_tile(3, wf_grp[3])
+
+        wf_4 = regroup_wf_tile(4, on_vector)
+        fuse_tile(0, 0)
+        wf_5 = regroup_wf_tile(5, on_scalar)
+        quantise_wf_tile(5, wf_5)
+        quantise_wf_tile(4, wf_4)
+        fuse_tile(1, 0)
+        fuse_tile(2, 0)
+        wf_6 = regroup_wf_tile(6, on_vector)
+        fuse_tile(0, 1)
+        wf_7 = regroup_wf_tile(7, on_scalar)
+        quantise_wf_tile(7, wf_7)
+        quantise_wf_tile(6, wf_6)
+        fuse_tile(1, 1)
+        fuse_tile(2, 1)
         for i in range(WF_AHEAD, N_TILES):
-            if i + 1 < N_TILES:
-                wf_grp.append(regroup_wf_tile(i + 1))
-            quantise_wf_tile(i, wf_grp[i])
             for b in range(B):
                 fuse_tile(i, b)

@@ -23,6 +23,9 @@ DT = 1024
 DA = 1024
 F = DT + DA
 T_TILES = LT // P
+HALVES = 2
+BOTH = range(HALVES)
+SIDE = T_TILES // HALVES
 N_TILES = DT // P
 G_ALL = F // K_PASS
 G_TGT = DT // K_PASS
@@ -72,7 +75,10 @@ def tile_informationfusion_pb_kernel(tc, scores, auxiliary, target, Wf, b_f, out
             nc.sync.dma_start(out=aux_raw[b][:], in_=auxiliary[b].rearrange("(s p) d -> p s d", p=P))
 
         def load_target(b):
-            nc.sync.dma_start(out=tgt_raw[b][:], in_=target[b].rearrange("(p tt) k -> p (tt k)", tt=T_TILES))
+            nc.sync.dma_start(
+                out=tgt_raw[b][:].rearrange("p (h vk) -> p h vk", h=HALVES),
+                in_=target[b].rearrange("(h p v) k -> p h (v k)", h=HALVES, v=SIDE),
+            )
 
         def load_wf(half):
             n_cols = slice(half * WF_HALF, (half + 1) * WF_HALF)
@@ -85,13 +91,19 @@ def tile_informationfusion_pb_kernel(tc, scores, auxiliary, target, Wf, b_f, out
                 else:
                     nc.sync.dma_start(out=wf_raw[half][:, g, :, :], in_=rows.rearrange("(s p) n -> p s n", p=P))
 
-        by_partition = [scores[b].rearrange("(p tt) a -> p tt a", tt=T_TILES) for b in range(B)]
-        for tt in range(T_TILES):
-            nc.sync.dma_start(out=sc_raw[0][:, tt, :], in_=by_partition[0][:, tt, :])
+        def load_scores(b, h):
+            nc.sync.dma_start(
+                out=sc_raw[b][:, h * SIDE : (h + 1) * SIDE, :].rearrange("p v a -> p (v a)"),
+                in_=scores[b, h * SIDE * P : (h + 1) * SIDE * P, :].rearrange("(p v) a -> p (v a)", v=SIDE),
+            )
+
+        for h in range(HALVES):
+            load_scores(0, h)
         load_auxiliary(0)
         nc.sync.dma_start(out=bias_rows[0:N_TILES, :], in_=b_f.rearrange("(i c) -> i c", c=P))
         load_target(0)
-        nc.sync.dma_start(out=sc_raw[1][:], in_=by_partition[1])
+        for h in range(HALVES):
+            load_scores(1, h)
         load_auxiliary(1)
         load_wf(0)
         load_target(1)
@@ -259,28 +271,30 @@ def tile_informationfusion_pb_kernel(tc, scores, auxiliary, target, Wf, b_f, out
         def quantise_wf_tile(i, wf_grp):
             nc.vector.quantize_mx(out=wf_codes[:, i, :].bitcast(FP8X4), scales=wf_scales[:, i, :], in_=wf_grp[:])
 
-        def fuse_tile(i, b):
-            acc = psum.tile([P, LT], F32, tag="bank")
+        def fuse_tile(i, b, halves):
+            count = len(halves) * SIDE * P
+            t_cols = slice(halves[0] * SIDE * P, halves[0] * SIDE * P + count)
+            acc = psum.tile([P, count], F32, tag="bank")
             for g in range(G_ALL):
                 n_cols = slice(g * P, (g + 1) * P)
                 nc.tensor.matmul_mx(
                     out=acc[:],
                     lhsT=wf_codes[:, i, n_cols].bitcast(FP8X4),
                     lhsT_scale=wf_scales[:, i, n_cols],
-                    rhs=x_codes[b][:, g, :].bitcast(FP8X4),
-                    rhs_scale=x_scales[b][:, g, :],
+                    rhs=x_codes[b][:, g, t_cols].bitcast(FP8X4),
+                    rhs_scale=x_scales[b][:, g, t_cols],
                     start=(g == 0),
                     stop=(g == G_ALL - 1),
                 )
-            y = result.tile([P, LT], F32)
+            y = result.tile([P, count], F32)
             nc.scalar.activation(
-                out=y[:].rearrange("n (p tt) -> n p tt", tt=T_TILES),
-                in_=acc[:].rearrange("n (tt p) -> n p tt", tt=T_TILES),
+                out=y[:].rearrange("n (h p v) -> n h p v", p=P, v=SIDE),
+                in_=acc[:].rearrange("n (h v p) -> n h p v", v=SIDE, p=P),
                 func=ACT.Tanh,
                 bias=bias_col[:, i : i + 1],
                 scale=1.0,
             )
-            nc.sync.dma_start(out=out[b, i * P : (i + 1) * P, :], in_=y[:])
+            nc.sync.dma_start(out=out[b, i * P : (i + 1) * P, t_cols], in_=y[:])
 
         on_vector, on_scalar = nc.vector.tensor_copy, nc.scalar.copy
 
@@ -298,66 +312,69 @@ def tile_informationfusion_pb_kernel(tc, scores, auxiliary, target, Wf, b_f, out
         quantise_auxiliary(0, 0, aux_0)
         at_grp = [regroup_attention(at_ps[tt]) for tt in range(T_TILES)]
         quantise_auxiliary(0, 1, aux_1)
-        for tt in range(T_TILES):
-            quantise_attention(0, tt, at_grp[tt])
         target_0 = transpose_target(0)
         bias_ps = transpose_bias()
 
-        halve_rows(1, 0)
-        halve_rows(1, 1)
-        quantise_x(0, 0, target_0[0])
-        halve_rows(1, 2)
+        quantise_attention(0, 0, at_grp[0])
+        for j in range(HALVINGS):
+            quantise_attention(0, j + 1, at_grp[j + 1])
+            halve_rows(1, j)
         nc.vector.tensor_copy(out=bias_col[:], in_=bias_ps[:, 0:N_TILES])
         row_max_of_halved(1)
+        quantise_x(0, 0, target_0[0])
         sums_0 = pool(0, 0)
         sums_1 = pool(0, 1)
         e = [exponentiate(1, tt) for tt in range(T_TILES)]
         pooled_0 = regroup_pooled(sums_0)
         aux_0 = regroup_auxiliary(1, 0, on_vector)
-        quantise_x(0, 1, target_0[1])
         aux_1 = regroup_auxiliary(1, 1, on_vector)
         nc.vector.reciprocal(out=inv_sum[:, T_TILES : 2 * T_TILES], in_=row_sum[:, T_TILES : 2 * T_TILES])
         quantise_auxiliary(1, 0, aux_0)
         at_ps = [normalise(1, tt, e[tt]) for tt in range(T_TILES)]
         quantise_auxiliary(1, 1, aux_1)
-        wf_grp = [regroup_wf_tile(0, on_vector)]
+        quantise_x(0, 1, target_0[1])
         at_grp = [regroup_attention(at_ps[tt]) for tt in range(T_TILES)]
         for tt in range(T_TILES):
             quantise_attention(1, tt, at_grp[tt])
+        wf_grp = [regroup_wf_tile(0, on_vector)]
         pooled_1 = regroup_pooled(sums_1)
         wf_grp.append(regroup_wf_tile(1, on_vector))
         quantise_wf_tile(0, wf_grp[0])
         quantise_x(0, G_TGT, pooled_0)
         quantise_x(0, G_TGT + 1, pooled_1)
         quantise_wf_tile(1, wf_grp[1])
-        target_1 = transpose_target(1)
         sums_0 = pool(1, 0)
-        pooled_0 = regroup_pooled(sums_0)
         sums_1 = pool(1, 1)
+        pooled_0 = regroup_pooled(sums_0)
         pooled_1 = regroup_pooled(sums_1)
+        target_1 = transpose_target(1)
         wf_grp.append(regroup_wf_tile(2, on_vector))
+        quantise_x(1, G_TGT, pooled_0)
+        quantise_wf_tile(2, wf_grp[2])
+        quantise_x(1, G_TGT + 1, pooled_1)
         quantise_x(1, 0, target_1[0])
         quantise_x(1, 1, target_1[1])
-        quantise_wf_tile(2, wf_grp[2])
         wf_grp.append(regroup_wf_tile(3, on_vector))
-        quantise_x(1, G_TGT, pooled_0)
-        quantise_x(1, G_TGT + 1, pooled_1)
-        quantise_wf_tile(3, wf_grp[3])
 
         wf_4 = regroup_wf_tile(4, on_vector)
-        fuse_tile(0, 0)
+        quantise_wf_tile(3, wf_grp[3])
+        fuse_tile(0, 0, BOTH)
         wf_5 = regroup_wf_tile(5, on_scalar)
         quantise_wf_tile(5, wf_5)
         quantise_wf_tile(4, wf_4)
-        fuse_tile(1, 0)
-        fuse_tile(2, 0)
+        fuse_tile(1, 0, BOTH)
+        fuse_tile(2, 0, BOTH)
         wf_6 = regroup_wf_tile(6, on_vector)
-        fuse_tile(0, 1)
+        fuse_tile(0, 1, BOTH)
         wf_7 = regroup_wf_tile(7, on_scalar)
         quantise_wf_tile(7, wf_7)
         quantise_wf_tile(6, wf_6)
-        fuse_tile(1, 1)
-        fuse_tile(2, 1)
+        fuse_tile(1, 1, BOTH)
+        fuse_tile(2, 1, BOTH)
         for i in range(WF_AHEAD, N_TILES):
             for b in range(B):
-                fuse_tile(i, b)
+                if (i, b) == (N_TILES - 1, B - 1):
+                    for h in BOTH:
+                        fuse_tile(i, b, [h])
+                else:
+                    fuse_tile(i, b, BOTH)

@@ -35,6 +35,7 @@ WF_HALF = DT // 2
 WF_AHEAD = 3
 HALVINGS = 3
 PSUM_BANKS = 8
+MX_ALIGN = 256
 
 FLOPS = 2 * B * LT * LA * DA + 2 * B * LT * F * DT
 
@@ -111,14 +112,14 @@ def tile_informationfusion_pb_kernel(tc, scores, auxiliary, target, Wf, b_f, out
 
         at_codes, at_scales, aux_codes, aux_scales, x_codes, x_scales = [], [], [], [], [], []
         for b in range(B):
-            at_codes.append(keep.tile([P, LT], U32, name="at_codes%d" % b, align_bytes=64))
-            at_scales.append(keep.tile([P, LT], U8, name="at_scales%d" % b, align_bytes=64))
-            aux_codes.append(keep.tile([P, DA], U32, name="aux_codes%d" % b, align_bytes=64))
-            aux_scales.append(keep.tile([P, DA], U8, name="aux_scales%d" % b, align_bytes=64))
-            x_codes.append(keep.tile([P, G_ALL, LT], U32, name="x_codes%d" % b, align_bytes=64))
-            x_scales.append(keep.tile([P, G_ALL, LT], U8, name="x_scales%d" % b, align_bytes=64))
-        wf_codes = keep.tile([P, N_TILES, G_ALL * P], U32, align_bytes=64)
-        wf_scales = keep.tile([P, N_TILES, G_ALL * P], U8, align_bytes=64)
+            at_codes.append(keep.tile([P, LT], U32, name="at_codes%d" % b, align_bytes=MX_ALIGN))
+            at_scales.append(keep.tile([P, LT], U8, name="at_scales%d" % b, align_bytes=MX_ALIGN))
+            aux_codes.append(keep.tile([P, DA], U32, name="aux_codes%d" % b, align_bytes=MX_ALIGN))
+            aux_scales.append(keep.tile([P, DA], U8, name="aux_scales%d" % b, align_bytes=MX_ALIGN))
+            x_codes.append(keep.tile([P, G_ALL, LT], U32, name="x_codes%d" % b, align_bytes=MX_ALIGN))
+            x_scales.append(keep.tile([P, G_ALL, LT], U8, name="x_scales%d" % b, align_bytes=MX_ALIGN))
+        wf_codes = keep.tile([P, N_TILES, G_ALL * P], U32, align_bytes=MX_ALIGN)
+        wf_scales = keep.tile([P, N_TILES, G_ALL * P], U8, align_bytes=MX_ALIGN)
 
         neg_max = const.tile([P, B * T_TILES], F32)
         row_sum = const.tile([P, B * T_TILES], F32)

@@ -32,6 +32,9 @@ G_TGT = DT // K_PASS
 G_AUX = DA // K_PASS
 RUN = 4
 WF_HALF = DT // 2
+TGT_PASSES = range(G_TGT)
+AUX_PASSES = range(G_TGT, G_ALL)
+ALL_PASSES = range(G_ALL)
 WF_AHEAD = 3
 HALVINGS = 3
 PSUM_BANKS = 8
@@ -272,11 +275,15 @@ def tile_informationfusion_pb_kernel(tc, scores, auxiliary, target, Wf, b_f, out
         def quantise_wf_tile(i, wf_grp):
             nc.vector.quantize_mx(out=wf_codes[:, i, :].bitcast(FP8X4), scales=wf_scales[:, i, :], in_=wf_grp[:])
 
-        def fuse_tile(i, b, halves):
+        def columns(halves):
             count = len(halves) * SIDE * P
-            t_cols = slice(halves[0] * SIDE * P, halves[0] * SIDE * P + count)
-            acc = psum.tile([P, count], F32, tag="bank")
-            for g in range(G_ALL):
+            return slice(halves[0] * SIDE * P, halves[0] * SIDE * P + count), count
+
+        def multiply(acc, i, b, halves, passes, start, stop):
+            t_cols, count = columns(halves)
+            if start:
+                acc = psum.tile([P, count], F32, tag="bank", name="acc")
+            for g in passes:
                 n_cols = slice(g * P, (g + 1) * P)
                 nc.tensor.matmul_mx(
                     out=acc[:],
@@ -284,10 +291,14 @@ def tile_informationfusion_pb_kernel(tc, scores, auxiliary, target, Wf, b_f, out
                     lhsT_scale=wf_scales[:, i, n_cols],
                     rhs=x_codes[b][:, g, t_cols].bitcast(FP8X4),
                     rhs_scale=x_scales[b][:, g, t_cols],
-                    start=(g == 0),
-                    stop=(g == G_ALL - 1),
+                    start=start and g == passes[0],
+                    stop=stop and g == passes[-1],
                 )
-            y = result.tile([P, count], F32)
+            return acc
+
+        def finish(acc, i, b, halves):
+            t_cols, count = columns(halves)
+            y = result.tile([P, count], F32, name="y")
             nc.scalar.activation(
                 out=y[:].rearrange("n (h p v) -> n h p v", p=P, v=SIDE),
                 in_=acc[:].rearrange("n (h v p) -> n h p v", v=SIDE, p=P),
@@ -296,6 +307,9 @@ def tile_informationfusion_pb_kernel(tc, scores, auxiliary, target, Wf, b_f, out
                 scale=1.0,
             )
             nc.sync.dma_start(out=out[b, i * P : (i + 1) * P, t_cols], in_=y[:])
+
+        def fuse_tile(i, b, halves):
+            finish(multiply(None, i, b, halves, ALL_PASSES, True, True), i, b, halves)
 
         on_vector, on_scalar = nc.vector.tensor_copy, nc.scalar.copy
 
@@ -354,8 +368,8 @@ def tile_informationfusion_pb_kernel(tc, scores, auxiliary, target, Wf, b_f, out
         quantise_wf_tile(2, wf_grp[2])
         quantise_x(1, G_TGT + 1, pooled_1)
         quantise_x(1, 0, target_1[0])
-        quantise_x(1, 1, target_1[1])
         wf_grp.append(regroup_wf_tile(3, on_vector))
+        quantise_x(1, 1, target_1[1])
 
         wf_4 = regroup_wf_tile(4, on_vector)
         quantise_wf_tile(3, wf_grp[3])
@@ -366,12 +380,15 @@ def tile_informationfusion_pb_kernel(tc, scores, auxiliary, target, Wf, b_f, out
         fuse_tile(1, 0, BOTH)
         fuse_tile(2, 0, BOTH)
         wf_6 = regroup_wf_tile(6, on_vector)
-        fuse_tile(0, 1, BOTH)
+        acc = [multiply(None, i, 1, BOTH, AUX_PASSES, True, False) for i in range(WF_AHEAD)]
+        for i in range(WF_AHEAD):
+            multiply(acc[i], i, 1, BOTH, TGT_PASSES, False, True)
+        finish(acc[0], 0, 1, BOTH)
         wf_7 = regroup_wf_tile(7, on_scalar)
         quantise_wf_tile(7, wf_7)
         quantise_wf_tile(6, wf_6)
-        fuse_tile(1, 1, BOTH)
-        fuse_tile(2, 1, BOTH)
+        finish(acc[1], 1, 1, BOTH)
+        finish(acc[2], 2, 1, BOTH)
         for i in range(WF_AHEAD, N_TILES):
             for b in range(B):
                 if (i, b) == (N_TILES - 1, B - 1):

@@ -30,7 +30,7 @@ N_TILES = DT // P
 G_ALL = F // K_PASS
 G_TGT = DT // K_PASS
 G_AUX = DA // K_PASS
-RUN = 4
+RUN = 8
 WF_HALF = DT // 2
 TGT_PASSES = range(G_TGT)
 AUX_PASSES = range(G_TGT, G_ALL)

@@ -347,15 +347,15 @@ def tile_informationfusion_pb_kernel(tc, scores, auxiliary, target, Wf, b_f, out
         quantise_auxiliary(1, 0, aux_0)
         at_ps = [normalise(1, tt, e[tt]) for tt in range(T_TILES)]
         quantise_auxiliary(1, 1, aux_1)
-        quantise_x(0, 1, target_0[1])
+        quantise_x(0, G_TGT, pooled_0)
         at_grp = [regroup_attention(at_ps[tt]) for tt in range(T_TILES)]
         for tt in range(T_TILES):
             quantise_attention(1, tt, at_grp[tt])
+        quantise_x(0, 1, target_0[1])
         wf_grp = [regroup_wf_tile(0, on_vector)]
         pooled_1 = regroup_pooled(sums_1)
         wf_grp.append(regroup_wf_tile(1, on_vector))
         quantise_wf_tile(0, wf_grp[0])
-        quantise_x(0, G_TGT, pooled_0)
         quantise_x(0, G_TGT + 1, pooled_1)
         quantise_wf_tile(1, wf_grp[1])
         sums_0 = pool(1, 0)

@@ -242,10 +242,10 @@ def tile_informationfusion_pb_kernel(tc, scores, auxiliary, target, Wf, b_f, out
                 out=x_codes[b][:, g, :].bitcast(FP8X4), scales=x_scales[b][:, g, :], in_=x_grp[:]
             )
 
-        def transpose_target(b):
+        def transpose_target(b, gs=range(G_TGT)):
             words = tgt_raw[b][:].bitcast(F32)
             groups = []
-            for g in range(G_TGT):
+            for g in gs:
                 tg_grp = grp.tile([P, LT * PACK], BF16, name="tg_grp", align_bytes=64)
                 tg_words = tg_grp[:].bitcast(F32)
                 for h in range(T_TILES // 2):
@@ -338,7 +338,6 @@ def tile_informationfusion_pb_kernel(tc, scores, auxiliary, target, Wf, b_f, out
         row_max_of_halved(1)
         quantise_x(0, 0, target_0[0])
         sums_0 = pool(0, 0)
-        sums_1 = pool(0, 1)
         e = [exponentiate(1, tt) for tt in range(T_TILES)]
         pooled_0 = regroup_pooled(sums_0)
         aux_0 = regroup_auxiliary(1, 0, on_vector)
@@ -346,6 +345,7 @@ def tile_informationfusion_pb_kernel(tc, scores, auxiliary, target, Wf, b_f, out
         nc.vector.reciprocal(out=inv_sum[:, T_TILES : 2 * T_TILES], in_=row_sum[:, T_TILES : 2 * T_TILES])
         quantise_auxiliary(1, 0, aux_0)
         at_ps = [normalise(1, tt, e[tt]) for tt in range(T_TILES)]
+        sums_1 = pool(0, 1)
         quantise_auxiliary(1, 1, aux_1)
         quantise_x(0, G_TGT, pooled_0)
         at_grp = [regroup_attention(at_ps[tt]) for tt in range(T_TILES)]
@@ -362,33 +362,27 @@ def tile_informationfusion_pb_kernel(tc, scores, auxiliary, target, Wf, b_f, out
         sums_1 = pool(1, 1)
         pooled_0 = regroup_pooled(sums_0)
         pooled_1 = regroup_pooled(sums_1)
-        target_1 = transpose_target(1)
+        target_1 = transpose_target(1, [0])
+        acc_0 = multiply(None, 0, 0, BOTH, ALL_PASSES, True, True)
+        target_1 += transpose_target(1, [1])
         wf_grp.append(regroup_wf_tile(2, on_vector))
-        quantise_x(1, G_TGT, pooled_0)
         quantise_wf_tile(2, wf_grp[2])
+        quantise_x(1, G_TGT, pooled_0)
         quantise_x(1, G_TGT + 1, pooled_1)
         quantise_x(1, 0, target_1[0])
-        wf_grp.append(regroup_wf_tile(3, on_vector))
         quantise_x(1, 1, target_1[1])
+        wf_grp.append(regroup_wf_tile(3, on_scalar))
 
-        wf_4 = regroup_wf_tile(4, on_vector)
-        quantise_wf_tile(3, wf_grp[3])
-        fuse_tile(0, 0, BOTH)
-        wf_5 = regroup_wf_tile(5, on_scalar)
-        quantise_wf_tile(5, wf_5)
-        quantise_wf_tile(4, wf_4)
+        finish(acc_0, 0, 0, BOTH)
         fuse_tile(1, 0, BOTH)
         fuse_tile(2, 0, BOTH)
-        wf_6 = regroup_wf_tile(6, on_vector)
         acc = [multiply(None, i, 1, BOTH, AUX_PASSES, True, False) for i in range(WF_AHEAD)]
         for i in range(WF_AHEAD):
-            multiply(acc[i], i, 1, BOTH, TGT_PASSES, False, True)
-        finish(acc[0], 0, 1, BOTH)
-        wf_7 = regroup_wf_tile(7, on_scalar)
-        quantise_wf_tile(7, wf_7)
-        quantise_wf_tile(6, wf_6)
-        finish(acc[1], 1, 1, BOTH)
-        finish(acc[2], 2, 1, BOTH)
+            finish(multiply(acc[i], i, 1, BOTH, TGT_PASSES, False, True), i, 1, BOTH)
+        for i in range(4, N_TILES):
+            wf_grp.append(regroup_wf_tile(i, on_vector))
+            quantise_wf_tile(i - 1, wf_grp[i - 1])
+        quantise_wf_tile(N_TILES - 1, wf_grp[N_TILES - 1])
         for i in range(WF_AHEAD, N_TILES):
             for b in range(B):
                 if (i, b) == (N_TILES - 1, B - 1):

from contextlib import ExitStack

import concourse.mybir as mybir
from concourse.masks import make_identity

BF16 = mybir.dt.bfloat16
F32 = mybir.dt.float32
U32 = mybir.dt.uint32
U8 = mybir.dt.uint8
FP8X4 = mybir.dt.float8_e4m3fn_x4
ACT = mybir.ActivationFunctionType
ALU = mybir.AluOpType
AXIS = mybir.AxisListType

P = 128
PACK = 4
K_PASS = P * PACK

B = 2
LT = 512
LA = 512
DT = 1024
DA = 1024
F = DT + DA
T_TILES = LT // P
HALVES = 2
BOTH = range(HALVES)
SIDE = T_TILES // HALVES
N_TILES = DT // P
G_ALL = F // K_PASS
G_TGT = DT // K_PASS
G_AUX = DA // K_PASS
RUN = 8
WF_HALF = DT // 2
TGT_PASSES = range(G_TGT)
AUX_PASSES = range(G_TGT, G_ALL)
ALL_PASSES = range(G_ALL)
WF_AHEAD = 3
HALVINGS = 3
PSUM_BANKS = 8
MX_ALIGN = 256

FLOPS = 2 * B * LT * LA * DA + 2 * B * LT * F * DT


def tile_informationfusion_pb_kernel(tc, scores, auxiliary, target, Wf, b_f, out):
    nc = tc.nc
    with ExitStack() as ctx:
        const = ctx.enter_context(tc.tile_pool(name="const", bufs=1))
        raw = ctx.enter_context(tc.tile_pool(name="raw", bufs=1))
        keep = ctx.enter_context(tc.tile_pool(name="keep", bufs=1))
        soft = ctx.enter_context(tc.tile_pool(name="soft", bufs=T_TILES))
        grp = ctx.enter_context(tc.tile_pool(name="grp", bufs=4))
        pooled_grp = ctx.enter_context(tc.tile_pool(name="pooled_grp", bufs=B * G_AUX))
        result = ctx.enter_context(tc.tile_pool(name="result", bufs=8))
        psum = ctx.enter_context(tc.psum_pool(name="psum", bufs=PSUM_BANKS))
        ctx.enter_context(tc.manual_schedule())

        ident_bf = const.tile([P, P], BF16)
        make_identity(nc, ident_bf[:])
        ident_f32 = const.tile([P, P], F32)
        make_identity(nc, ident_f32[:])
        bias_rows = const.tile([P, P], BF16)
        nc.vector.memset(bias_rows[:], 0.0)
        warm = const.tile([P, 2], F32)
        nc.vector.memset(warm[:], 0.0)
        nc.scalar.activation(out=warm[:, 1:2], in_=warm[:, 0:1], func=ACT.Exp)

        sc_raw = []
        aux_raw = []
        tgt_raw = []
        for b in range(B):
            sc_raw.append(raw.tile([P, T_TILES, LA], BF16, name="sc_raw%d" % b))
            aux_raw.append(raw.tile([P, PACK, DA], BF16, name="aux_raw%d" % b))
            tgt_raw.append(raw.tile([P, T_TILES * DT], BF16, name="tgt_raw%d" % b))
        wf_raw = [raw.tile([P, G_ALL, PACK, WF_HALF], BF16, name="wf_raw%d" % h) for h in range(2)]

        def load_auxiliary(b):
            nc.sync.dma_start(out=aux_raw[b][:], in_=auxiliary[b].rearrange("(s p) d -> p s d", p=P))

        def load_target(b):
            nc.sync.dma_start(
                out=tgt_raw[b][:].rearrange("p (h vk) -> p h vk", h=HALVES),
                in_=target[b].rearrange("(h p v) k -> p h (v k)", h=HALVES, v=SIDE),
            )

        def load_wf(half):
            n_cols = slice(half * WF_HALF, (half + 1) * WF_HALF)
            for g in range(G_ALL):
                rows = Wf[g * K_PASS : (g + 1) * K_PASS, n_cols]
                if g < G_TGT:
                    pairs = rows.rearrange("(u p e) n -> p u e n", p=P, e=2)
                    for u in range(2):
                        nc.sync.dma_start(out=wf_raw[half][:, g, 2 * u : 2 * u + 2, :], in_=pairs[:, u, :, :])
                else:
                    nc.sync.dma_start(out=wf_raw[half][:, g, :, :], in_=rows.rearrange("(s p) n -> p s n", p=P))

        def load_scores(b, h):
            nc.sync.dma_start(
                out=sc_raw[b][:, h * SIDE : (h + 1) * SIDE, :].rearrange("p v a -> p (v a)"),
                in_=scores[b, h * SIDE * P : (h + 1) * SIDE * P, :].rearrange("(p v) a -> p (v a)", v=SIDE),
            )

        for h in range(HALVES):
            load_scores(0, h)
        load_auxiliary(0)
        nc.sync.dma_start(out=bias_rows[0:N_TILES, :], in_=b_f.rearrange("(i c) -> i c", c=P))
        load_target(0)
        for h in range(HALVES):
            load_scores(1, h)
        load_auxiliary(1)
        load_wf(0)
        load_target(1)
        load_wf(1)

        at_codes, at_scales, aux_codes, aux_scales, x_codes, x_scales = [], [], [], [], [], []
        for b in range(B):
            at_codes.append(keep.tile([P, LT], U32, name="at_codes%d" % b, align_bytes=MX_ALIGN))
            at_scales.append(keep.tile([P, LT], U8, name="at_scales%d" % b, align_bytes=MX_ALIGN))
            aux_codes.append(keep.tile([P, DA], U32, name="aux_codes%d" % b, align_bytes=MX_ALIGN))
            aux_scales.append(keep.tile([P, DA], U8, name="aux_scales%d" % b, align_bytes=MX_ALIGN))
            x_codes.append(keep.tile([P, G_ALL, LT], U32, name="x_codes%d" % b, align_bytes=MX_ALIGN))
            x_scales.append(keep.tile([P, G_ALL, LT], U8, name="x_scales%d" % b, align_bytes=MX_ALIGN))
        wf_codes = keep.tile([P, N_TILES, G_ALL * P], U32, align_bytes=MX_ALIGN)
        wf_scales = keep.tile([P, N_TILES, G_ALL * P], U8, align_bytes=MX_ALIGN)

        neg_max = const.tile([P, B * T_TILES], F32)
        row_sum = const.tile([P, B * T_TILES], F32)
        inv_sum = const.tile([P, B * T_TILES], F32)
        bias_col = const.tile([P, N_TILES], F32)
        halved = [const.tile([P, T_TILES, LA >> (j + 1)], BF16, name="halved%d" % j) for j in range(HALVINGS)]

        def stat(b, tt):
            return slice(b * T_TILES + tt, b * T_TILES + tt + 1)

        def transpose_bias():
            bias_ps = psum.tile([P, P], BF16, tag="bank")
            nc.tensor.transpose(bias_ps[:], bias_rows[:], ident_bf[:])
            return bias_ps

        def row_max(b, tt):
            nc.vector.tensor_reduce(
                out=neg_max[:, stat(b, tt)], in_=sc_raw[b][:, tt, :], axis=AXIS.X, op=ALU.max, negate=True
            )

        def halve_rows(b, j):
            rows = sc_raw[b] if j == 0 else halved[j - 1]
            width = LA >> (j + 1)
            nc.vector.tensor_tensor(
                out=halved[j][:], in0=rows[:, :, 0:width], in1=rows[:, :, width : 2 * width], op=ALU.max
            )

        def row_max_of_halved(b):
            nc.vector.tensor_reduce(
                out=neg_max[:, b * T_TILES : (b + 1) * T_TILES],
                in_=halved[HALVINGS - 1][:],
                axis=AXIS.X,
                op=ALU.max,
                negate=True,
            )

        def exponentiate(b, tt):
            e = soft.tile([P, LA], F32, name="e")
            nc.scalar.activation(
                out=e[:],
                in_=sc_raw[b][:, tt, :],
                func=ACT.Exp,
                bias=neg_max[:, stat(b, tt)],
                scale=1.0,
                accum_out=row_sum[:, stat(b, tt)],
            )
            return e

        def normalise(b, tt, e):
            attn = soft.tile([P, LA], BF16, name="attn")
            nc.vector.tensor_scalar(
                out=attn[:], in0=e[:], scalar1=inv_sum[:, stat(b, tt)], scalar2=None, op0=ALU.mult
            )
            at_ps = psum.tile([P, PACK, P], BF16, tag="bank", name="at_ps")
            for s in range(PACK):
                nc.tensor.transpose(at_ps[:, s, :], attn[:, s * P : (s + 1) * P], ident_bf[:])
            return at_ps

        def regroup_attention(bank):
            at_grp = soft.tile([P, P * PACK], BF16, name="at_grp", align_bytes=64)
            nc.scalar.copy(
                out=at_grp[:].rearrange("p (t s) -> p t s", s=PACK), in_=bank[:].rearrange("p s t -> p t s")
            )
            return at_grp

        def quantise_attention(b, tt, at_grp):
            t_cols = slice(tt * P, (tt + 1) * P)
            nc.vector.quantize_mx(
                out=at_codes[b][:, t_cols].bitcast(FP8X4), scales=at_scales[b][:, t_cols], in_=at_grp[:]
            )

        def regroup_auxiliary(b, q, copy):
            d_cols = slice(q * K_PASS, (q + 1) * K_PASS)
            aux_grp = grp.tile([P, K_PASS * PACK], BF16, name="aux_grp", align_bytes=64)
            copy(
                out=aux_grp[:].rearrange("p (c r s) -> p c s r", r=RUN, s=PACK),
                in_=aux_raw[b][:, :, d_cols].rearrange("p s (c r) -> p c s r", r=RUN),
            )
            return aux_grp

        def quantise_auxiliary(b, q, aux_grp):
            d_cols = slice(q * K_PASS, (q + 1) * K_PASS)
            nc.vector.quantize_mx(
                out=aux_codes[b][:, d_cols].bitcast(FP8X4), scales=aux_scales[b][:, d_cols], in_=aux_grp[:]
            )

        def pool(b, q):
            banks = []
            for tt in range(T_TILES):
                t_cols = slice(tt * P, (tt + 1) * P)
                wa_ps = psum.tile([P, PACK, P], F32, tag="bank", name="wa_ps")
                for s in range(PACK):
                    d_cols = slice((q * PACK + s) * P, (q * PACK + s + 1) * P)
                    nc.tensor.matmul_mx(
                        out=wa_ps[:, s, :],
                        lhsT=aux_codes[b][:, d_cols].bitcast(FP8X4),
                        lhsT_scale=aux_scales[b][:, d_cols],
                        rhs=at_codes[b][:, t_cols].bitcast(FP8X4),
                        rhs_scale=at_scales[b][:, t_cols],
                        start=True,
                        stop=True,
                    )
                banks.append(wa_ps)
            return banks

        def regroup_pooled(banks):
            pooled = pooled_grp.tile([P, LT * PACK], BF16, name="pooled", align_bytes=64)
            for tt in range(T_TILES):
                nc.scalar.copy(
                    out=pooled[:, tt * K_PASS : (tt + 1) * K_PASS].rearrange("p (t s) -> p t s", s=PACK),
                    in_=banks[tt][:].rearrange("p s t -> p t s"),
                )
            return pooled

        def quantise_x(b, g, x_grp):
            nc.vector.quantize_mx(
                out=x_codes[b][:, g, :].bitcast(FP8X4), scales=x_scales[b][:, g, :], in_=x_grp[:]
            )

        def transpose_target(b, gs=range(G_TGT)):
            words = tgt_raw[b][:].bitcast(F32)
            groups = []
            for g in gs:
                tg_grp = grp.tile([P, LT * PACK], BF16, name="tg_grp", align_bytes=64)
                tg_words = tg_grp[:].bitcast(F32)
                for h in range(T_TILES // 2):
                    tg_ps = psum.tile([P, 2, 2 * P], F32, tag="bank", name="tg_ps")
                    for u in range(2):
                        for v in range(2):
                            first = (2 * h + v) * (DT // 2) + (2 * g + u) * P
                            nc.tensor.transpose(
                                tg_ps[:, u, v * P : (v + 1) * P], words[:, first : first + P], ident_f32[:]
                            )
                    nc.scalar.copy(
                        out=tg_words[:, h * 4 * P : (h + 1) * 4 * P].rearrange("p (t u) -> p t u", u=2),
                        in_=tg_ps[:].rearrange("p u t -> p t u"),
                    )
                groups.append(tg_grp)
            return groups

        def regroup_wf_tile(i, copy):
            half, first = divmod(i * P, WF_HALF)
            wf_grp = grp.tile([P, G_ALL * P * PACK], BF16, name="wf_grp", align_bytes=64)
            copy(
                out=wf_grp[:].rearrange("p (g c r s) -> p g c s r", g=G_ALL, r=RUN, s=PACK),
                in_=wf_raw[half][:, :, :, first : first + P].rearrange("p g s (c r) -> p g c s r", r=RUN),
            )
            return wf_grp

        def quantise_wf_tile(i, wf_grp):
            nc.vector.quantize_mx(out=wf_codes[:, i, :].bitcast(FP8X4), scales=wf_scales[:, i, :], in_=wf_grp[:])

        def columns(halves):
            count = len(halves) * SIDE * P
            return slice(halves[0] * SIDE * P, halves[0] * SIDE * P + count), count

        def multiply(acc, i, b, halves, passes, start, stop):
            t_cols, count = columns(halves)
            if start:
                acc = psum.tile([P, count], F32, tag="bank", name="acc")
            for g in passes:
                n_cols = slice(g * P, (g + 1) * P)
                nc.tensor.matmul_mx(
                    out=acc[:],
                    lhsT=wf_codes[:, i, n_cols].bitcast(FP8X4),
                    lhsT_scale=wf_scales[:, i, n_cols],
                    rhs=x_codes[b][:, g, t_cols].bitcast(FP8X4),
                    rhs_scale=x_scales[b][:, g, t_cols],
                    start=start and g == passes[0],
                    stop=stop and g == passes[-1],
                )
            return acc

        def finish(acc, i, b, halves):
            t_cols, count = columns(halves)
            y = result.tile([P, count], F32, name="y")
            nc.scalar.activation(
                out=y[:].rearrange("n (h p v) -> n h p v", p=P, v=SIDE),
                in_=acc[:].rearrange("n (h v p) -> n h p v", v=SIDE, p=P),
                func=ACT.Tanh,
                bias=bias_col[:, i : i + 1],
                scale=1.0,
            )
            nc.sync.dma_start(out=out[b, i * P : (i + 1) * P, t_cols], in_=y[:])

        def fuse_tile(i, b, halves):
            finish(multiply(None, i, b, halves, ALL_PASSES, True, True), i, b, halves)

        on_vector, on_scalar = nc.vector.tensor_copy, nc.scalar.copy

        e, at_ps = {}, {}
        for j in range(T_TILES + 3):
            if j < T_TILES:
                row_max(0, j)
                e[j] = exponentiate(0, j)
            if 0 <= j - 2 < T_TILES:
                nc.vector.reciprocal(out=inv_sum[:, stat(0, j - 2)], in_=row_sum[:, stat(0, j - 2)])
            if 0 <= j - 3 < T_TILES:
                at_ps[j - 3] = normalise(0, j - 3, e[j - 3])
        aux_0 = regroup_auxiliary(0, 0, on_vector)
        aux_1 = regroup_auxiliary(0, 1, on_scalar)
        quantise_auxiliary(0, 0, aux_0)
        at_grp = [regroup_attention(at_ps[tt]) for tt in range(T_TILES)]
        quantise_auxiliary(0, 1, aux_1)
        target_0 = transpose_target(0)
        bias_ps = transpose_bias()

        quantise_attention(0, 0, at_grp[0])
        for j in range(HALVINGS):
            quantise_attention(0, j + 1, at_grp[j + 1])
            halve_rows(1, j)
        nc.vector.tensor_copy(out=bias_col[:], in_=bias_ps[:, 0:N_TILES])
        row_max_of_halved(1)
        quantise_x(0, 0, target_0[0])
        sums_0 = pool(0, 0)
        e = [exponentiate(1, tt) for tt in range(T_TILES)]
        pooled_0 = regroup_pooled(sums_0)
        aux_0 = regroup_auxiliary(1, 0, on_vector)
        aux_1 = regroup_auxiliary(1, 1, on_vector)
        nc.vector.reciprocal(out=inv_sum[:, T_TILES : 2 * T_TILES], in_=row_sum[:, T_TILES : 2 * T_TILES])
        quantise_auxiliary(1, 0, aux_0)
        at_ps = [normalise(1, tt, e[tt]) for tt in range(T_TILES)]
        sums_1 = pool(0, 1)
        quantise_auxiliary(1, 1, aux_1)
        quantise_x(0, G_TGT, pooled_0)
        at_grp = [regroup_attention(at_ps[tt]) for tt in range(T_TILES)]
        for tt in range(T_TILES):
            quantise_attention(1, tt, at_grp[tt])
        quantise_x(0, 1, target_0[1])
        wf_grp = [regroup_wf_tile(0, on_vector)]
        pooled_1 = regroup_pooled(sums_1)
        wf_grp.append(regroup_wf_tile(1, on_vector))
        quantise_wf_tile(0, wf_grp[0])
        quantise_x(0, G_TGT + 1, pooled_1)
        quantise_wf_tile(1, wf_grp[1])
        sums_0 = pool(1, 0)
        sums_1 = pool(1, 1)
        pooled_0 = regroup_pooled(sums_0)
        pooled_1 = regroup_pooled(sums_1)
        target_1 = transpose_target(1, [0])
        acc_0 = multiply(None, 0, 0, BOTH, ALL_PASSES, True, True)
        target_1 += transpose_target(1, [1])
        wf_grp.append(regroup_wf_tile(2, on_vector))
        quantise_wf_tile(2, wf_grp[2])
        quantise_x(1, G_TGT, pooled_0)
        quantise_x(1, G_TGT + 1, pooled_1)
        quantise_x(1, 0, target_1[0])
        quantise_x(1, 1, target_1[1])
        wf_grp.append(regroup_wf_tile(3, on_scalar))

        finish(acc_0, 0, 0, BOTH)
        fuse_tile(1, 0, BOTH)
        fuse_tile(2, 0, BOTH)
        acc = [multiply(None, i, 1, BOTH, AUX_PASSES, True, False) for i in range(WF_AHEAD)]
        for i in range(WF_AHEAD):
            finish(multiply(acc[i], i, 1, BOTH, TGT_PASSES, False, True), i, 1, BOTH)
        for i in range(4, N_TILES):
            wf_grp.append(regroup_wf_tile(i, on_vector))
            quantise_wf_tile(i - 1, wf_grp[i - 1])
        quantise_wf_tile(N_TILES - 1, wf_grp[N_TILES - 1])
        for i in range(WF_AHEAD, N_TILES):
            for b in range(B):
                if (i, b) == (N_TILES - 1, B - 1):
                    for h in BOTH:
                        fuse_tile(i, b, [h])
                else:
                    fuse_tile(i, b, BOTH)
